import numpy as np
import ml_dtypes


def mxq(x, axis, fmt="e4m3"):
    dtype, down = {"e4m3": (ml_dtypes.float8_e4m3fn, 7), "e5m2": (ml_dtypes.float8_e5m2, 14)}[fmt]
    v = np.moveaxis(np.asarray(x, np.float32).astype(ml_dtypes.bfloat16).astype(np.float64), axis, -1)
    blocks = v.reshape(v.shape[:-1] + (-1, 32))
    amax = np.abs(blocks).max(-1, keepdims=True)
    byte = np.maximum(np.where(amax > 0, np.frexp(amax)[1] - 1 + 127, 0) - down, 1)
    scale = np.exp2(byte - 127.0)
    codes = (blocks / scale).astype(np.float32).astype(dtype).astype(np.float64)
    return np.moveaxis((codes * scale).reshape(v.shape), -1, axis)


WIDE = False


def mx_kscale(k):
    if not WIDE:
        return np.ones(k)
    levels = np.array([10, -10, 5, -5, 0])
    if k % 512:
        return np.exp2(np.random.permutation(np.resize(levels, k // 32))).repeat(32)
    a = np.empty((k // 512, 16))
    for p in range(k // 512):
        a[p, :8] = np.random.permutation(np.resize(levels, 8))
        for g in range(8):
            far = levels[np.abs(levels - a[p, g]) >= 10]
            a[p, g + 8] = far[np.random.randint(len(far))]
    return np.exp2(a.ravel()).repeat(32)


BF16 = ml_dtypes.bfloat16


def bf(x):
    return np.asarray(x, np.float32).astype(BF16)


def f64(x):
    return np.asarray(x).astype(np.float64)


B, C, H, W, DM, GH = 6, 1024, 16, 16, 128, 1024
OFFSETS = [(-4, -4), (-4, -1), (-4, 2), (-3, 4), (-2, -3), (2, 3), (3, -2), (4, 4)]
N = len(OFFSETS)


def setup_inputs():
    s = mx_kscale(C)
    e = np.exp(0.7 * np.random.standard_normal((N, B)))
    return {'x': bf(np.random.standard_normal((B, C, H, W)) * s[None, :, None, None]),
            'mw': bf(np.random.standard_normal((C, C)) * 2.0 / np.sqrt(C) / s[None, :]),
            'mb': bf(np.random.standard_normal(C) * 0.3),
            'attn_w': bf(e / e.sum(0, keepdims=True))}


def reference(x, mw, mb, attn_w):
    xq = mxq(f64(x).reshape(B, C, H * W), 1, 'e4m3')
    m = (mxq(f64(mw), 1, 'e4m3') @ xq).reshape(B, C, H, W) + f64(mb)[None, :, None, None]
    wts = f64(attn_w)
    agg = np.zeros_like(m)
    for i, (dy, dx) in enumerate(OFFSETS):
        agg = agg + np.roll(m, (dy, dx), axis=(2, 3)) * wts[i][:, None, None, None]
    return agg

@@ -1,0 +1,342 @@
+from contextlib import ExitStack
+
+from concourse import mybir
+from concourse.masks import make_identity
+
+F32 = mybir.dt.float32
+BF16 = mybir.dt.bfloat16
+U32 = mybir.dt.uint32
+U8 = mybir.dt.uint8
+FP8X4 = mybir.dt.float8_e4m3fn_x4
+ACT = mybir.ActivationFunctionType
+ALU = mybir.AluOpType
+
+P = 128
+PACK = 4
+K_PASS = P * PACK
+BANK = 512
+
+B, C, H, W = 6, 1024, 16, 16
+PIX = H * W
+HALF_ROWS = H // 2
+PASSES = C // K_PASS
+D_TILES = C // P
+OFFSETS = [(-4, -4), (-4, -1), (-4, 2), (-3, 4), (-2, -3), (2, 3), (3, -2), (4, 4)]
+TERMS = len(OFFSETS)
+REACH = 4
+GROUP = 4
+GROUPS = D_TILES // GROUP
+
+FLOPS = 2 * B * C * C * PIX + 2 * TERMS * B * C * PIX
+
+
+def by_matrix(b):
+    return b % 3 != 0
+
+
+def tile_graphaugmentation_pa_kernel(tc, x, mw, mb, attn_w, out):
+    nc = tc.nc
+    matrix_images = [b for b in range(B) if by_matrix(b)]
+    with ExitStack() as stack:
+        const = stack.enter_context(tc.tile_pool(name="const", bufs=1))
+        keep = stack.enter_context(tc.tile_pool(name="keep", bufs=1))
+        stage = stack.enter_context(tc.tile_pool(name="stage", bufs=2))
+        work = stack.enter_context(tc.tile_pool(name="work", bufs=4))
+        psum = stack.enter_context(tc.psum_pool(name="psum", bufs=8))
+        stack.enter_context(tc.manual_schedule())
+
+        x_raw = [keep.tile([P, PASSES * PACK * PIX], BF16, name="x_raw%d" % b) for b in range(B)]
+        mw_raw = keep.tile([P, D_TILES, C], BF16)
+
+        def load_x(b):
+            nc.sync.dma_start(
+                out=x_raw[b][:].rearrange("q (g r) -> q g r", g=PASSES),
+                in_=x[b].rearrange("(g q t) h w -> q g (t h w)", q=P, t=PACK),
+            )
+
+        w_bf = const.tile([P, TERMS * B], BF16)
+        nc.sync.dma_start(out=w_bf[:], in_=attn_w.rearrange("i b -> (i b)").partition_broadcast(P))
+        mb_rows = const.tile([P, P], BF16)
+        nc.vector.memset(mb_rows[:], 0.0)
+        nc.sync.dma_start(out=mb_rows[0:D_TILES, :], in_=mb.rearrange("(t p) -> t p", p=P))
+
+        load_x(0)
+        for pair in range(D_TILES // 2):
+            nc.sync.dma_start(
+                out=mw_raw[:, 2 * pair : 2 * pair + 2, :],
+                in_=mw[2 * pair * P : (2 * pair + 2) * P, :].rearrange("(t p) c -> p t c", p=P),
+            )
+        for b in range(1, B):
+            load_x(b)
+
+        ident = const.tile([P, P], F32)
+        make_identity(nc, ident[:])
+        w_f32 = const.tile([P, TERMS * B], F32)
+        nc.vector.tensor_copy(out=w_f32[:], in_=w_bf[:])
+
+        mb_rows_f32 = const.tile([P, P], F32)
+        nc.vector.tensor_copy(out=mb_rows_f32[:], in_=mb_rows[:])
+        mb_t = psum.tile([P, BANK], F32, tag="bank")
+        nc.tensor.transpose(mb_t[:, 0:P], mb_rows_f32[:], ident[:])
+
+        def weight(i, b):
+            return w_f32[:, i * B + b : i * B + b + 1]
+
+        def shifted(ring, i, rows):
+            dy, dx = OFFSETS[i]
+            return ring[:, REACH - dy : REACH - dy + rows, :, (-dx) % W : (-dx) % W + W]
+
+        def first_term(ring, rows, n, b):
+            acc = work.tile([P, rows, n, W], F32, name="acc%dx%d" % (rows, n))
+            nc.scalar.activation(out=acc[:], in_=shifted(ring, 0, rows), func=ACT.Copy, scale=weight(0, b))
+            return (ring, rows, n, b, acc)
+
+        def other_terms(chains):
+            for i in range(1, TERMS - 1):
+                for ring, rows, n, b, acc, res in chains:
+                    nc.vector.scalar_tensor_tensor(
+                        out=acc[:], in0=shifted(ring, i, rows), scalar=weight(i, b), in1=acc[:],
+                        op0=ALU.mult, op1=ALU.add,
+                    )
+            for ring, rows, n, b, acc, res in chains:
+                for j in range(n):
+                    nc.vector.scalar_tensor_tensor(
+                        out=res[:, j, :].rearrange("p (h w) -> p h w", w=W),
+                        in0=shifted(ring, TERMS - 1, rows)[:, :, j, :],
+                        scalar=weight(TERMS - 1, b),
+                        in1=acc[:, :, j, :],
+                        op0=ALU.mult,
+                        op1=ALU.add,
+                    )
+
+        fold_ring = const.tile([P, HALF_ROWS + 2 * REACH, 2, 2 * W], F32)
+        for ring_row, image_row, n, over_the_edge in [
+            (0, HALF_ROWS - REACH, REACH, True),
+            (REACH, 0, HALF_ROWS, False),
+            (REACH + HALF_ROWS, 0, REACH, True),
+        ]:
+            for sign in range(2):
+                nc.vector.tensor_scalar_mul(
+                    out=fold_ring[:, ring_row : ring_row + n, sign, :].rearrange("p r (c w) -> p r c w", c=2),
+                    in0=ident[:, image_row * W : (image_row + n) * W]
+                    .rearrange("p (r w) -> p r w", w=W)
+                    .unsqueeze(2)
+                    .to_broadcast([P, n, 2, W]),
+                    scalar1=(-0.5 if over_the_edge and sign == 1 else 0.5),
+                )
+        matrix = dict((b, const.tile([P, 2, P], F32, name="matrix%d" % b)) for b in matrix_images)
+        matrix_chains = [first_term(fold_ring, HALF_ROWS, 2, b) + (matrix[b],) for b in matrix_images]
+        other_terms(matrix_chains[:2])
+
+        mb_sb = const.tile([P, D_TILES], F32)
+        nc.vector.tensor_copy(out=mb_sb[:], in_=mb_t[:, 0:D_TILES])
+        w_sum = const.tile([P, B], F32)
+        nc.vector.reduce_sum(out=w_sum[:], in_=w_f32[:].rearrange("p (i b) -> p b i", b=B), axis=mybir.AxisListType.X)
+        mb_w = dict((b, const.tile([P, D_TILES], F32, name="mb_w%d" % b)) for b in matrix_images)
+        for b in matrix_images:
+            nc.vector.tensor_scalar_mul(out=mb_w[b][:], in0=mb_sb[:], scalar1=w_sum[:, b : b + 1])
+
+        x_codes = [keep.tile([P, PASSES, PIX], U32, name="x_codes%d" % b, align_bytes=64) for b in range(B)]
+        x_scales = [keep.tile([P, PASSES, PIX], U8, name="x_scales%d" % b, align_bytes=64) for b in range(B)]
+        minus_codes = dict((b, keep.tile([P, PASSES, P], U32, name="minus_codes%d" % b, align_bytes=64)) for b in matrix_images)
+        minus_scales = dict((b, keep.tile([P, PASSES, P], U8, name="minus_scales%d" % b, align_bytes=64)) for b in matrix_images)
+
+        grouped = dict()
+
+        def regroup_x(b):
+            on_vector = b < B - 2
+            rows_of_words = x_raw[b][:].rearrange("q (g t c) -> q g t c", g=PASSES, t=PACK)
+            x_grp = stage.tile([P, PASSES, PIX * PACK], BF16, align_bytes=64)
+            copy = nc.vector.tensor_copy if on_vector else nc.scalar.copy
+            for g in range(PASSES):
+                copy(
+                    out=x_grp[:, g, :].rearrange("q (c i t) -> q c t i", i=4, t=PACK),
+                    in_=rows_of_words[:, g, :, :].rearrange("q t (c i) -> q c t i", i=4),
+                )
+            grouped[b] = [(x_grp, x_codes[b], x_scales[b])]
+            if by_matrix(b):
+                minus_grp = stage.tile([P, PASSES, P * PACK], BF16, align_bytes=64)
+                for g in range(PASSES):
+                    to = minus_grp[:, g, :].rearrange("q (c i t) -> q c t i", i=4, t=PACK)
+                    upper = rows_of_words[:, g, :, P : 2 * P].rearrange("q t (c i) -> q c t i", i=4)
+                    if on_vector:
+                        nc.vector.tensor_scalar_mul(out=to, in0=upper, scalar1=-1.0)
+                    else:
+                        nc.scalar.mul(out=to, in_=upper, mul=-1.0)
+                grouped[b].append((minus_grp, minus_codes[b], minus_scales[b]))
+
+        def quantise_x(b):
+            for values, codes, scales in grouped[b]:
+                nc.vector.quantize_mx(
+                    out=codes[:].rearrange("q g c -> q (g c)").bitcast(FP8X4),
+                    scales=scales[:].rearrange("q g c -> q (g c)"),
+                    in_=values[:].rearrange("q g c -> q (g c)"),
+                )
+
+        regroup_x(0)
+        quantise_x(0)
+
+        mw_codes = keep.tile([P, PASSES, C], U32, align_bytes=64)
+        mw_scales = keep.tile([P, PASSES, C], U8, align_bytes=64)
+        for t in range(D_TILES):
+            words = mw_raw[:, t, :].bitcast(F32)
+            w_t = psum.tile([P, BANK], F32, tag="bank")
+            for g in range(PASSES):
+                for u in range(2):
+                    nc.tensor.transpose(
+                        w_t[:, (2 * g + u) * P : (2 * g + u + 1) * P],
+                        words[:, 2 * P * g + u : 2 * P * (g + 1) : 2],
+                        ident[:],
+                    )
+            mw_grp = stage.tile([P, PASSES * P * PACK], BF16, align_bytes=64)
+            nc.scalar.copy(
+                out=mw_grp[:].bitcast(F32).rearrange("q (g d u) -> q g d u", g=PASSES, u=2),
+                in_=w_t[:].rearrange("q (g u d) -> q g d u", g=PASSES, u=2),
+            )
+            for g in range(PASSES):
+                nc.vector.quantize_mx(
+                    out=mw_codes[:, g, t * P : (t + 1) * P].bitcast(FP8X4),
+                    scales=mw_scales[:, g, t * P : (t + 1) * P],
+                    in_=mw_grp[:, g * P * PACK : (g + 1) * P * PACK],
+                )
+
+        regroup_x(1)
+        quantise_x(1)
+
+        def mw_part(g, channels):
+            return (mw_codes[:, g, channels], mw_scales[:, g, channels])
+
+        def x_part(b, g, pixels):
+            return (x_codes[b][:, g, pixels], x_scales[b][:, g, pixels])
+
+        def minus_part(b, g):
+            return (minus_codes[b][:, g, :], minus_scales[b][:, g, :])
+
+        def mx_group(acc, pairs):
+            for k, (still, moving) in enumerate(pairs):
+                nc.tensor.matmul_mx(
+                    out=acc,
+                    lhsT=still[0].bitcast(FP8X4),
+                    lhsT_scale=still[1],
+                    rhs=moving[0].bitcast(FP8X4),
+                    rhs_scale=moving[1],
+                    start=(k == 0),
+                    stop=(k == len(pairs) - 1),
+                )
+
+        def store(b, grp, res):
+            nc.sync.dma_start(
+                out=out[b, grp * GROUP * P : (grp + 1) * GROUP * P].rearrange("(j p) h w -> p j (h w)", p=P),
+                in_=res[:],
+            )
+
+        def multiply_direct(b):
+            chains = []
+            for grp in range(GROUPS):
+                ring = work.tile([P, H + 2 * REACH, GROUP, 2 * W], F32, name="ring")
+                for j in range(GROUP):
+                    t = grp * GROUP + j
+                    channels = slice(t * P, (t + 1) * P)
+                    bank = psum.tile([P, BANK], F32, tag="bank")
+                    for at, first, n in [(0, PIX // 2, PIX // 2), (PIX // 2, 0, PIX), (PIX // 2 + PIX, 0, PIX // 2)]:
+                        mx_group(
+                            bank[:, at : at + n],
+                            [(mw_part(g, channels), x_part(b, g, slice(first, first + n))) for g in range(PASSES)],
+                        )
+                    rows = bank[:, (HALF_ROWS - REACH) * W : (HALF_ROWS + H + REACH) * W]
+                    nc.scalar.activation(
+                        out=ring[:, :, j, :].rearrange("p r (c w) -> p r c w", c=2),
+                        in_=rows.rearrange("p (r w) -> p r w", w=W).unsqueeze(2).to_broadcast([P, H + 2 * REACH, 2, W]),
+                        func=ACT.Identity,
+                        bias=mb_sb[:, t : t + 1],
+                        scale=1.0,
+                    )
+                chains.append(first_term(ring, H, GROUP, b))
+            return chains
+
+        def finish_direct(b, chains):
+            results = [work.tile([P, GROUP, PIX], F32, name="res") for chain in chains]
+            other_terms([chain + (res,) for chain, res in zip(chains, results)])
+            for grp, res in enumerate(results):
+                store(b, grp, res)
+
+        def multiply_folded(b):
+            folded = work.tile([P, 2, C], F32, name="folded", bufs=2)
+            for sign in range(2):
+                for n in range(C // BANK):
+                    channels = slice(n * BANK, (n + 1) * BANK)
+                    bank = psum.tile([P, BANK], F32, tag="bank")
+                    lower = [(x_part(b, g, slice(0, P)), mw_part(g, channels)) for g in range(PASSES)]
+                    upper = [
+                        (x_part(b, g, slice(P, 2 * P)) if sign == 0 else minus_part(b, g), mw_part(g, channels))
+                        for g in range(PASSES)
+                    ]
+                    mx_group(bank[:], lower + upper)
+                    nc.scalar.copy(out=folded[:, sign, channels], in_=bank[:])
+            return folded
+
+        def apply_matrices(b, folded):
+            parts = []
+            for grp in range(GROUPS):
+                bank_u = psum.tile([P, BANK], F32, tag="bank")
+                bank_v = psum.tile([P, BANK], F32, tag="bank")
+                for sign, bank in enumerate((bank_u, bank_v)):
+                    for j in range(GROUP):
+                        t = grp * GROUP + j
+                        nc.tensor.matmul(
+                            out=bank[:, j * P : (j + 1) * P],
+                            lhsT=folded[:, sign, t * P : (t + 1) * P],
+                            rhs=matrix[b][:, sign, :],
+                            start=True,
+                            stop=True,
+                        )
+                u_sb = work.tile([P, GROUP, P], F32, name="u_sb")
+                for j in range(GROUP):
+                    t = grp * GROUP + j
+                    nc.scalar.activation(
+                        out=u_sb[:, j, :],
+                        in_=bank_u[:, j * P : (j + 1) * P],
+                        func=ACT.Identity,
+                        bias=mb_w[b][:, t : t + 1],
+                        scale=1.0,
+                    )
+                parts.append((u_sb, bank_v))
+            return parts
+
+        def finish_by_matrix(b, parts):
+            for grp, (u_sb, bank_v) in enumerate(parts):
+                res = work.tile([P, GROUP, PIX], F32, name="res")
+                for half, sign in enumerate((1.0, -1.0)):
+                    nc.vector.scalar_tensor_tensor(
+                        out=res[:, :, half * P : (half + 1) * P],
+                        in0=bank_v[:].rearrange("p (j c) -> p j c", j=GROUP),
+                        scalar=sign,
+                        in1=u_sb[:],
+                        op0=ALU.mult,
+                        op1=ALU.add,
+                    )
+                store(b, grp, res)
+
+        def multiply(b):
+            return multiply_folded(b) if by_matrix(b) else multiply_direct(b)
+
+        products = dict()
+        products[0] = multiply(0)
+        other_terms(matrix_chains[2:])
+        for b in (2, 3):
+            regroup_x(b)
+            quantise_x(b)
+        products[1] = multiply(1)
+        for b in range(B):
+            if b + 4 < B:
+                regroup_x(b + 4)
+            if b + 2 < B:
+                products[b + 2] = multiply(b + 2)
+            if b + 1 < B and by_matrix(b + 1):
+                products[b + 1] = apply_matrices(b + 1, products[b + 1])
+            if by_matrix(b):
+                finish_by_matrix(b, products[b])
+            else:
+                finish_direct(b, products[b])
+            if b + 4 < B:
+                quantise_x(b + 4)

@@ -25,13 +25,19 @@ OFFSETS = [(-4, -4), (-4, -1), (-4, 2), (-3, 4), (-2, -3), (2, 3), (3, -2), (4, 
 TERMS = len(OFFSETS)
 REACH = 4
 GROUP = 4
-GROUPS = D_TILES // GROUP
 
 FLOPS = 2 * B * C * C * PIX + 2 * TERMS * B * C * PIX
 
 
+DIRECT_TILES = (8, 0, 0, 2, 0, 0)
+
+
 def by_matrix(b):
-    return b % 3 != 0
+    return DIRECT_TILES[b] < D_TILES
+
+
+def tile_groups(first, last):
+    return [(t, min(GROUP, last - t)) for t in range(first, last, GROUP)]
 
 
 def tile_graphaugmentation_pa_kernel(tc, x, mw, mb, attn_w, out):
@@ -87,7 +93,7 @@ def tile_graphaugmentation_pa_kernel(tc, x, mw, mb, attn_w, out):
             return ring[:, REACH - dy : REACH - dy + rows, :, (-dx) % W : (-dx) % W + W]
 
         def first_term(ring, rows, n, b):
-            acc = work.tile([P, rows, n, W], F32, name="acc%dx%d" % (rows, n))
+            acc = work.tile([P, rows, n, W], F32, name="acc%dx%d" % (rows, n), bufs=4 if n == 2 else 2)
             nc.scalar.activation(out=acc[:], in_=shifted(ring, 0, rows), func=ACT.Copy, scale=weight(0, b))
             return (ring, rows, n, b, acc)
 
@@ -224,18 +230,18 @@ def tile_graphaugmentation_pa_kernel(tc, x, mw, mb, attn_w, out):
                     stop=(k == len(pairs) - 1),
                 )
 
-        def store(b, grp, res):
+        def store(b, t0, n, res):
             nc.sync.dma_start(
-                out=out[b, grp * GROUP * P : (grp + 1) * GROUP * P].rearrange("(j p) h w -> p j (h w)", p=P),
+                out=out[b, t0 * P : (t0 + n) * P].rearrange("(j p) h w -> p j (h w)", p=P),
                 in_=res[:],
             )
 
         def multiply_direct(b):
             chains = []
-            for grp in range(GROUPS):
-                ring = work.tile([P, H + 2 * REACH, GROUP, 2 * W], F32, name="ring")
-                for j in range(GROUP):
-                    t = grp * GROUP + j
+            for t0, n_tiles in tile_groups(D_TILES - DIRECT_TILES[b], D_TILES):
+                ring = work.tile([P, H + 2 * REACH, n_tiles, 2 * W], F32, name="ring%d" % n_tiles, bufs=2)
+                for j in range(n_tiles):
+                    t = t0 + j
                     channels = slice(t * P, (t + 1) * P)
                     bank = psum.tile([P, BANK], F32, tag="bank")
                     for at, first, n in [(0, PIX // 2, PIX // 2), (PIX // 2, 0, PIX), (PIX // 2 + PIX, 0, PIX // 2)]:
@@ -251,38 +257,39 @@ def tile_graphaugmentation_pa_kernel(tc, x, mw, mb, attn_w, out):
                         bias=mb_sb[:, t : t + 1],
                         scale=1.0,
                     )
-                chains.append(first_term(ring, H, GROUP, b))
+                chains.append(first_term(ring, H, n_tiles, b))
             return chains
 
         def finish_direct(b, chains):
-            results = [work.tile([P, GROUP, PIX], F32, name="res") for chain in chains]
+            groups = tile_groups(D_TILES - DIRECT_TILES[b], D_TILES)
+            results = [work.tile([P, n, PIX], F32, name="res%d" % n) for t0, n in groups]
             other_terms([chain + (res,) for chain, res in zip(chains, results)])
-            for grp, res in enumerate(results):
-                store(b, grp, res)
+            for (t0, n), res in zip(groups, results):
+                store(b, t0, n, res)
 
         def multiply_folded(b):
             folded = work.tile([P, 2, C], F32, name="folded", bufs=2)
             for sign in range(2):
-                for n in range(C // BANK):
-                    channels = slice(n * BANK, (n + 1) * BANK)
+                for t0, n_tiles in tile_groups(0, D_TILES - DIRECT_TILES[b]):
+                    channels = slice(t0 * P, (t0 + n_tiles) * P)
                     bank = psum.tile([P, BANK], F32, tag="bank")
                     lower = [(x_part(b, g, slice(0, P)), mw_part(g, channels)) for g in range(PASSES)]
                     upper = [
                         (x_part(b, g, slice(P, 2 * P)) if sign == 0 else minus_part(b, g), mw_part(g, channels))
                         for g in range(PASSES)
                     ]
-                    mx_group(bank[:], lower + upper)
-                    nc.scalar.copy(out=folded[:, sign, channels], in_=bank[:])
+                    mx_group(bank[:, 0 : n_tiles * P], lower + upper)
+                    nc.scalar.copy(out=folded[:, sign, channels], in_=bank[:, 0 : n_tiles * P])
             return folded
 
         def apply_matrices(b, folded):
             parts = []
-            for grp in range(GROUPS):
+            for t0, n_tiles in tile_groups(0, D_TILES - DIRECT_TILES[b]):
                 bank_u = psum.tile([P, BANK], F32, tag="bank")
                 bank_v = psum.tile([P, BANK], F32, tag="bank")
                 for sign, bank in enumerate((bank_u, bank_v)):
-                    for j in range(GROUP):
-                        t = grp * GROUP + j
+                    for j in range(n_tiles):
+                        t = t0 + j
                         nc.tensor.matmul(
                             out=bank[:, j * P : (j + 1) * P],
                             lhsT=folded[:, sign, t * P : (t + 1) * P],
@@ -290,9 +297,9 @@ def tile_graphaugmentation_pa_kernel(tc, x, mw, mb, attn_w, out):
                             start=True,
                             stop=True,
                         )
-                u_sb = work.tile([P, GROUP, P], F32, name="u_sb")
-                for j in range(GROUP):
-                    t = grp * GROUP + j
+                u_sb = work.tile([P, n_tiles, P], F32, name="u_sb%d" % n_tiles)
+                for j in range(n_tiles):
+                    t = t0 + j
                     nc.scalar.activation(
                         out=u_sb[:, j, :],
                         in_=bank_u[:, j * P : (j + 1) * P],
@@ -300,43 +307,49 @@ def tile_graphaugmentation_pa_kernel(tc, x, mw, mb, attn_w, out):
                         bias=mb_w[b][:, t : t + 1],
                         scale=1.0,
                     )
-                parts.append((u_sb, bank_v))
+                parts.append((t0, n_tiles, u_sb, bank_v))
             return parts
 
         def finish_by_matrix(b, parts):
-            for grp, (u_sb, bank_v) in enumerate(parts):
-                res = work.tile([P, GROUP, PIX], F32, name="res")
+            for t0, n_tiles, u_sb, bank_v in parts:
+                res = work.tile([P, n_tiles, PIX], F32, name="res%d" % n_tiles)
                 for half, sign in enumerate((1.0, -1.0)):
                     nc.vector.scalar_tensor_tensor(
                         out=res[:, :, half * P : (half + 1) * P],
-                        in0=bank_v[:].rearrange("p (j c) -> p j c", j=GROUP),
+                        in0=bank_v[:, 0 : n_tiles * P].rearrange("p (j c) -> p j c", j=n_tiles),
                         scalar=sign,
                         in1=u_sb[:],
                         op0=ALU.mult,
                         op1=ALU.add,
                     )
-                store(b, grp, res)
+                store(b, t0, n_tiles, res)
+
+        folded = dict()
+        chains = dict()
+        parts = dict()
 
         def multiply(b):
-            return multiply_folded(b) if by_matrix(b) else multiply_direct(b)
+            if by_matrix(b):
+                folded[b] = multiply_folded(b)
+            if DIRECT_TILES[b] > 0:
+                chains[b] = multiply_direct(b)
 
-        products = dict()
-        products[0] = multiply(0)
+        multiply(0)
         other_terms(matrix_chains[2:])
         for b in (2, 3):
             regroup_x(b)
             quantise_x(b)
-        products[1] = multiply(1)
+        multiply(1)
         for b in range(B):
             if b + 4 < B:
                 regroup_x(b + 4)
             if b + 2 < B:
-                products[b + 2] = multiply(b + 2)
+                multiply(b + 2)
             if b + 1 < B and by_matrix(b + 1):
-                products[b + 1] = apply_matrices(b + 1, products[b + 1])
+                parts[b + 1] = apply_matrices(b + 1, folded[b + 1])
             if by_matrix(b):
-                finish_by_matrix(b, products[b])
-            else:
-                finish_direct(b, products[b])
+                finish_by_matrix(b, parts[b])
+            if DIRECT_TILES[b] > 0:
+                finish_direct(b, chains[b])
             if b + 4 < B:
                 quantise_x(b + 4)

@@ -25,9 +25,9 @@ OFFSETS = [(-4, -4), (-4, -1), (-4, 2), (-3, 4), (-2, -3), (2, 3), (3, -2), (4, 
 TERMS = len(OFFSETS)
 REACH = 4
 GROUP = 4
+PAIR = 2
 
 FLOPS = 2 * B * C * C * PIX + 2 * TERMS * B * C * PIX
-
 
 DIRECT_TILES = (8, 0, 0, 2, 0, 0)
 
@@ -36,8 +36,8 @@ def by_matrix(b):
     return DIRECT_TILES[b] < D_TILES
 
 
-def tile_groups(first, last):
-    return [(t, min(GROUP, last - t)) for t in range(first, last, GROUP)]
+def tile_groups(first, last, size):
+    return [(t, min(size, last - t)) for t in range(first, last, size)]
 
 
 def tile_graphaugmentation_pa_kernel(tc, x, mw, mb, attn_w, out):
@@ -47,7 +47,7 @@ def tile_graphaugmentation_pa_kernel(tc, x, mw, mb, attn_w, out):
         const = stack.enter_context(tc.tile_pool(name="const", bufs=1))
         keep = stack.enter_context(tc.tile_pool(name="keep", bufs=1))
         stage = stack.enter_context(tc.tile_pool(name="stage", bufs=2))
-        work = stack.enter_context(tc.tile_pool(name="work", bufs=4))
+        work = stack.enter_context(tc.tile_pool(name="work", bufs=2))
         psum = stack.enter_context(tc.psum_pool(name="psum", bufs=8))
         stack.enter_context(tc.manual_schedule())
 
@@ -77,6 +77,29 @@ def tile_graphaugmentation_pa_kernel(tc, x, mw, mb, attn_w, out):
 
         ident = const.tile([P, P], F32)
         make_identity(nc, ident[:])
+
+        half_ring = const.tile([P, HALF_ROWS + 2 * REACH, 2 * W], F32)
+        sign_ring = const.tile([P, HALF_ROWS + 2 * REACH, 2 * W], F32)
+        for ring_row, image_row, n, beyond in [
+            (0, HALF_ROWS - REACH, REACH, True),
+            (REACH, 0, HALF_ROWS, False),
+            (REACH + HALF_ROWS, 0, REACH, True),
+        ]:
+            rows = (
+                ident[:, image_row * W : (image_row + n) * W]
+                .rearrange("p (r w) -> p r w", w=W)
+                .unsqueeze(2)
+                .to_broadcast([P, n, 2, W])
+            )
+
+            def ring_rows(ring):
+                return ring[:, ring_row : ring_row + n, :].rearrange("p r (c w) -> p r c w", c=2)
+
+            nc.vector.tensor_scalar_mul(out=ring_rows(half_ring), in0=rows, scalar1=0.5)
+            nc.gpsimd.tensor_scalar(
+                out=ring_rows(sign_ring), in0=rows, scalar1=-1.0 if beyond else 1.0, scalar2=0.0, op0=ALU.mult, op1=ALU.add
+            )
+
         w_f32 = const.tile([P, TERMS * B], F32)
         nc.vector.tensor_copy(out=w_f32[:], in_=w_bf[:])
 
@@ -88,103 +111,86 @@ def tile_graphaugmentation_pa_kernel(tc, x, mw, mb, attn_w, out):
         def weight(i, b):
             return w_f32[:, i * B + b : i * B + b + 1]
 
-        def shifted(ring, i, rows):
+        def half_shifted(ring, i):
             dy, dx = OFFSETS[i]
-            return ring[:, REACH - dy : REACH - dy + rows, :, (-dx) % W : (-dx) % W + W]
+            return ring[:, REACH - dy : REACH - dy + HALF_ROWS, (-dx) % W : (-dx) % W + W]
 
-        def first_term(ring, rows, n, b):
-            acc = work.tile([P, rows, n, W], F32, name="acc%dx%d" % (rows, n), bufs=4 if n == 2 else 2)
-            nc.scalar.activation(out=acc[:], in_=shifted(ring, 0, rows), func=ACT.Copy, scale=weight(0, b))
-            return (ring, rows, n, b, acc)
+        def image_rows(matrix):
+            return matrix.rearrange("p (h w) -> p h w", w=W)
 
-        def other_terms(chains):
-            for i in range(1, TERMS - 1):
-                for ring, rows, n, b, acc, res in chains:
-                    nc.vector.scalar_tensor_tensor(
-                        out=acc[:], in0=shifted(ring, i, rows), scalar=weight(i, b), in1=acc[:],
-                        op0=ALU.mult, op1=ALU.add,
-                    )
-            for ring, rows, n, b, acc, res in chains:
-                for j in range(n):
-                    nc.vector.scalar_tensor_tensor(
-                        out=res[:, j, :].rearrange("p (h w) -> p h w", w=W),
-                        in0=shifted(ring, TERMS - 1, rows)[:, :, j, :],
-                        scalar=weight(TERMS - 1, b),
-                        in1=acc[:, :, j, :],
-                        op0=ALU.mult,
-                        op1=ALU.add,
-                    )
-
-        fold_ring = const.tile([P, HALF_ROWS + 2 * REACH, 2, 2 * W], F32)
-        for ring_row, image_row, n, over_the_edge in [
-            (0, HALF_ROWS - REACH, REACH, True),
-            (REACH, 0, HALF_ROWS, False),
-            (REACH + HALF_ROWS, 0, REACH, True),
-        ]:
-            for sign in range(2):
-                nc.vector.tensor_scalar_mul(
-                    out=fold_ring[:, ring_row : ring_row + n, sign, :].rearrange("p r (c w) -> p r c w", c=2),
-                    in0=ident[:, image_row * W : (image_row + n) * W]
-                    .rearrange("p (r w) -> p r w", w=W)
-                    .unsqueeze(2)
-                    .to_broadcast([P, n, 2, W]),
-                    scalar1=(-0.5 if over_the_edge and sign == 1 else 0.5),
-                )
+        edge_sign = const.tile([P, P], F32)
+        nc.gpsimd.tensor_tensor(
+            out=image_rows(edge_sign[:]), in0=half_shifted(sign_ring, 0), in1=half_shifted(sign_ring, 1), op=ALU.add
+        )
+        for i in range(2, TERMS):
+            nc.gpsimd.tensor_tensor(
+                out=image_rows(edge_sign[:]), in0=image_rows(edge_sign[:]), in1=half_shifted(sign_ring, i), op=ALU.add
+            )
         matrix = dict((b, const.tile([P, 2, P], F32, name="matrix%d" % b)) for b in matrix_images)
-        matrix_chains = [first_term(fold_ring, HALF_ROWS, 2, b) + (matrix[b],) for b in matrix_images]
-        other_terms(matrix_chains[:2])
-
-        mb_sb = const.tile([P, D_TILES], F32)
-        nc.vector.tensor_copy(out=mb_sb[:], in_=mb_t[:, 0:D_TILES])
-        w_sum = const.tile([P, B], F32)
-        nc.vector.reduce_sum(out=w_sum[:], in_=w_f32[:].rearrange("p (i b) -> p b i", b=B), axis=mybir.AxisListType.X)
-        mb_w = dict((b, const.tile([P, D_TILES], F32, name="mb_w%d" % b)) for b in matrix_images)
         for b in matrix_images:
-            nc.vector.tensor_scalar_mul(out=mb_w[b][:], in0=mb_sb[:], scalar1=w_sum[:, b : b + 1])
+            nc.scalar.activation(
+                out=image_rows(matrix[b][:, 0, :]), in_=half_shifted(half_ring, 0), func=ACT.Copy, scale=weight(0, b)
+            )
+
+        def matrix_term(b, i):
+            nc.vector.scalar_tensor_tensor(
+                out=image_rows(matrix[b][:, 0, :]),
+                in0=half_shifted(half_ring, i),
+                scalar=weight(i, b),
+                in1=image_rows(matrix[b][:, 0, :]),
+                op0=ALU.mult,
+                op1=ALU.add,
+            )
+            if i == TERMS - 1:
+                nc.gpsimd.tensor_tensor(out=matrix[b][:, 1, :], in0=matrix[b][:, 0, :], in1=edge_sign[:], op=ALU.mult)
+
+        matrix_steps = [(b, i) for i in range(1, TERMS) for b in matrix_images]
+
+        def build_matrices(steps):
+            for k in range(min(steps, len(matrix_steps))):
+                matrix_term(*matrix_steps[0])
+                matrix_steps.remove(matrix_steps[0])
 
         x_codes = [keep.tile([P, PASSES, PIX], U32, name="x_codes%d" % b, align_bytes=64) for b in range(B)]
         x_scales = [keep.tile([P, PASSES, PIX], U8, name="x_scales%d" % b, align_bytes=64) for b in range(B)]
         minus_codes = dict((b, keep.tile([P, PASSES, P], U32, name="minus_codes%d" % b, align_bytes=64)) for b in matrix_images)
         minus_scales = dict((b, keep.tile([P, PASSES, P], U8, name="minus_scales%d" % b, align_bytes=64)) for b in matrix_images)
-
         grouped = dict()
+        negated = dict()
 
-        def regroup_x(b):
-            on_vector = b < B - 2
-            rows_of_words = x_raw[b][:].rearrange("q (g t c) -> q g t c", g=PASSES, t=PACK)
-            x_grp = stage.tile([P, PASSES, PIX * PACK], BF16, align_bytes=64)
-            copy = nc.vector.tensor_copy if on_vector else nc.scalar.copy
+        def regroup_x(b, copy):
+            x_grp = stage.tile([P, PASSES, PIX * PACK], BF16, name="x_grp", align_bytes=64)
             for g in range(PASSES):
                 copy(
                     out=x_grp[:, g, :].rearrange("q (c i t) -> q c t i", i=4, t=PACK),
-                    in_=rows_of_words[:, g, :, :].rearrange("q t (c i) -> q c t i", i=4),
+                    in_=x_raw[b][:].rearrange("q (g t c i) -> q g c t i", g=PASSES, t=PACK, i=4)[:, g],
                 )
-            grouped[b] = [(x_grp, x_codes[b], x_scales[b])]
-            if by_matrix(b):
-                minus_grp = stage.tile([P, PASSES, P * PACK], BF16, align_bytes=64)
-                for g in range(PASSES):
-                    to = minus_grp[:, g, :].rearrange("q (c i t) -> q c t i", i=4, t=PACK)
-                    upper = rows_of_words[:, g, :, P : 2 * P].rearrange("q t (c i) -> q c t i", i=4)
-                    if on_vector:
-                        nc.vector.tensor_scalar_mul(out=to, in0=upper, scalar1=-1.0)
-                    else:
-                        nc.scalar.mul(out=to, in_=upper, mul=-1.0)
-                grouped[b].append((minus_grp, minus_codes[b], minus_scales[b]))
+            grouped[b] = x_grp
+
+        def negate_x(b):
+            minus_grp = stage.tile([P, PASSES, P * PACK], BF16, name="minus_grp", align_bytes=64)
+            nc.vector.tensor_scalar_mul(out=minus_grp[:], in0=grouped[b][:, :, P * PACK : 2 * P * PACK], scalar1=-1.0)
+            negated[b] = minus_grp
+
+        def quantise(values, codes, scales):
+            nc.vector.quantize_mx(
+                out=codes[:].rearrange("q g c -> q (g c)").bitcast(FP8X4),
+                scales=scales[:].rearrange("q g c -> q (g c)"),
+                in_=values[:].rearrange("q g c -> q (g c)"),
+            )
 
         def quantise_x(b):
-            for values, codes, scales in grouped[b]:
-                nc.vector.quantize_mx(
-                    out=codes[:].rearrange("q g c -> q (g c)").bitcast(FP8X4),
-                    scales=scales[:].rearrange("q g c -> q (g c)"),
-                    in_=values[:].rearrange("q g c -> q (g c)"),
-                )
-
-        regroup_x(0)
-        quantise_x(0)
+            if by_matrix(b):
+                negate_x(b)
+            quantise(grouped[b], x_codes[b], x_scales[b])
+            if by_matrix(b):
+                quantise(negated[b], minus_codes[b], minus_scales[b])
 
         mw_codes = keep.tile([P, PASSES, C], U32, align_bytes=64)
         mw_scales = keep.tile([P, PASSES, C], U8, align_bytes=64)
-        for t in range(D_TILES):
+        mw_grouped = dict()
+
+        def transpose_mw(t):
             words = mw_raw[:, t, :].bitcast(F32)
             w_t = psum.tile([P, BANK], F32, tag="bank")
             for g in range(PASSES):
@@ -194,20 +200,20 @@ def tile_graphaugmentation_pa_kernel(tc, x, mw, mb, attn_w, out):
                         words[:, 2 * P * g + u : 2 * P * (g + 1) : 2],
                         ident[:],
                     )
-            mw_grp = stage.tile([P, PASSES * P * PACK], BF16, align_bytes=64)
+            mw_grp = stage.tile([P, PASSES * P * PACK], BF16, name="mw_grp", align_bytes=64, bufs=4)
             nc.scalar.copy(
                 out=mw_grp[:].bitcast(F32).rearrange("q (g d u) -> q g d u", g=PASSES, u=2),
                 in_=w_t[:].rearrange("q (g u d) -> q g d u", g=PASSES, u=2),
             )
+            mw_grouped[t] = mw_grp
+
+        def quantise_mw(t):
             for g in range(PASSES):
                 nc.vector.quantize_mx(
                     out=mw_codes[:, g, t * P : (t + 1) * P].bitcast(FP8X4),
                     scales=mw_scales[:, g, t * P : (t + 1) * P],
-                    in_=mw_grp[:, g * P * PACK : (g + 1) * P * PACK],
+                    in_=mw_grouped[t][:, g * P * PACK : (g + 1) * P * PACK],
                 )
-
-        regroup_x(1)
-        quantise_x(1)
 
         def mw_part(g, channels):
             return (mw_codes[:, g, channels], mw_scales[:, g, channels])
@@ -236,41 +242,68 @@ def tile_graphaugmentation_pa_kernel(tc, x, mw, mb, attn_w, out):
                 in_=res[:],
             )
 
-        def multiply_direct(b):
-            chains = []
-            for t0, n_tiles in tile_groups(D_TILES - DIRECT_TILES[b], D_TILES):
-                ring = work.tile([P, H + 2 * REACH, n_tiles, 2 * W], F32, name="ring%d" % n_tiles, bufs=2)
-                for j in range(n_tiles):
-                    t = t0 + j
-                    channels = slice(t * P, (t + 1) * P)
-                    bank = psum.tile([P, BANK], F32, tag="bank")
-                    for at, first, n in [(0, PIX // 2, PIX // 2), (PIX // 2, 0, PIX), (PIX // 2 + PIX, 0, PIX // 2)]:
-                        mx_group(
-                            bank[:, at : at + n],
-                            [(mw_part(g, channels), x_part(b, g, slice(first, first + n))) for g in range(PASSES)],
-                        )
-                    rows = bank[:, (HALF_ROWS - REACH) * W : (HALF_ROWS + H + REACH) * W]
+        def shifted(ring, i):
+            dy, dx = OFFSETS[i]
+            return ring[:, REACH - dy : REACH - dy + H, :, (-dx) % W : (-dx) % W + W]
+
+        sum_steps = []
+
+        def add_term(chain, i):
+            b, t0, ring, acc, res = chain
+            if i < TERMS - 1:
+                nc.vector.scalar_tensor_tensor(
+                    out=acc[:], in0=shifted(ring, i), scalar=weight(i, b), in1=acc[:], op0=ALU.mult, op1=ALU.add
+                )
+                return
+            for j in range(PAIR):
+                nc.vector.scalar_tensor_tensor(
+                    out=res[:, j, :].rearrange("p (h w) -> p h w", w=W),
+                    in0=shifted(ring, i)[:, :, j, :],
+                    scalar=weight(i, b),
+                    in1=acc[:, :, j, :],
+                    op0=ALU.mult,
+                    op1=ALU.add,
+                )
+            store(b, t0, PAIR, res)
+
+        def direct_pair(b, t0):
+            ring = work.tile([P, H + 2 * REACH, PAIR, 2 * W], F32, name="ring", bufs=5)
+            bank = psum.tile([P, BANK], F32, tag="bank")
+            for j in range(PAIR):
+                t = t0 + j
+                channels = slice(t * P, (t + 1) * P)
+                acc = bank[:, j * PIX : (j + 1) * PIX]
+                mx_group(acc, [(mw_part(g, channels), x_part(b, g, slice(0, PIX))) for g in range(PASSES)])
+                for ring_row, image_row, n in [(REACH, 0, H), (0, H - REACH, REACH), (REACH + H, 0, REACH)]:
                     nc.scalar.activation(
-                        out=ring[:, :, j, :].rearrange("p r (c w) -> p r c w", c=2),
-                        in_=rows.rearrange("p (r w) -> p r w", w=W).unsqueeze(2).to_broadcast([P, H + 2 * REACH, 2, W]),
+                        out=ring[:, ring_row : ring_row + n, j, :].rearrange("p r (c w) -> p r c w", c=2),
+                        in_=acc[:, image_row * W : (image_row + n) * W]
+                        .rearrange("p (r w) -> p r w", w=W)
+                        .unsqueeze(2)
+                        .to_broadcast([P, n, 2, W]),
                         func=ACT.Identity,
                         bias=mb_sb[:, t : t + 1],
                         scale=1.0,
                     )
-                chains.append(first_term(ring, H, n_tiles, b))
-            return chains
+            first = work.tile([P, H, PAIR, W], F32, name="acc", bufs=5)
+            nc.scalar.activation(out=first[:], in_=shifted(ring, 0), func=ACT.Copy, scale=weight(0, b))
+            res = work.tile([P, PAIR, PIX], F32, name="res2", bufs=5)
+            return (b, t0, ring, first, res)
 
-        def finish_direct(b, chains):
-            groups = tile_groups(D_TILES - DIRECT_TILES[b], D_TILES)
-            results = [work.tile([P, n, PIX], F32, name="res%d" % n) for t0, n in groups]
-            other_terms([chain + (res,) for chain, res in zip(chains, results)])
-            for (t0, n), res in zip(groups, results):
-                store(b, t0, n, res)
+        def plan_sums(chains):
+            for i in range(1, TERMS):
+                for chain in chains:
+                    sum_steps.append((chain, i))
+
+        def add_terms(steps):
+            for k in range(min(steps, len(sum_steps))):
+                add_term(*sum_steps[0])
+                sum_steps.remove(sum_steps[0])
 
         def multiply_folded(b):
             folded = work.tile([P, 2, C], F32, name="folded", bufs=2)
             for sign in range(2):
-                for t0, n_tiles in tile_groups(0, D_TILES - DIRECT_TILES[b]):
+                for t0, n_tiles in tile_groups(0, D_TILES - DIRECT_TILES[b], GROUP):
                     channels = slice(t0 * P, (t0 + n_tiles) * P)
                     bank = psum.tile([P, BANK], F32, tag="bank")
                     lower = [(x_part(b, g, slice(0, P)), mw_part(g, channels)) for g in range(PASSES)]
@@ -282,74 +315,90 @@ def tile_graphaugmentation_pa_kernel(tc, x, mw, mb, attn_w, out):
                     nc.scalar.copy(out=folded[:, sign, channels], in_=bank[:, 0 : n_tiles * P])
             return folded
 
-        def apply_matrices(b, folded):
-            parts = []
-            for t0, n_tiles in tile_groups(0, D_TILES - DIRECT_TILES[b]):
-                bank_u = psum.tile([P, BANK], F32, tag="bank")
-                bank_v = psum.tile([P, BANK], F32, tag="bank")
-                for sign, bank in enumerate((bank_u, bank_v)):
-                    for j in range(n_tiles):
-                        t = t0 + j
-                        nc.tensor.matmul(
-                            out=bank[:, j * P : (j + 1) * P],
-                            lhsT=folded[:, sign, t * P : (t + 1) * P],
-                            rhs=matrix[b][:, sign, :],
-                            start=True,
-                            stop=True,
-                        )
-                u_sb = work.tile([P, n_tiles, P], F32, name="u_sb%d" % n_tiles)
+        def apply_matrices(b, folded, t0, n_tiles):
+            bank_u = psum.tile([P, BANK], F32, tag="bank")
+            bank_v = psum.tile([P, BANK], F32, tag="bank")
+            for sign, bank in enumerate((bank_u, bank_v)):
                 for j in range(n_tiles):
                     t = t0 + j
-                    nc.scalar.activation(
-                        out=u_sb[:, j, :],
-                        in_=bank_u[:, j * P : (j + 1) * P],
-                        func=ACT.Identity,
-                        bias=mb_w[b][:, t : t + 1],
-                        scale=1.0,
+                    nc.tensor.matmul(
+                        out=bank[:, j * P : (j + 1) * P],
+                        lhsT=folded[:, sign, t * P : (t + 1) * P],
+                        rhs=matrix[b][:, sign, :],
+                        start=True,
+                        stop=True,
                     )
-                parts.append((t0, n_tiles, u_sb, bank_v))
-            return parts
+            u_sb = work.tile([P, GROUP, P], F32, name="u_sb", bufs=3)
+            for j in range(n_tiles):
+                t = t0 + j
+                nc.scalar.activation(
+                    out=u_sb[:, j, :],
+                    in_=bank_u[:, j * P : (j + 1) * P],
+                    func=ACT.Identity,
+                    bias=mb_w[:, b, t : t + 1],
+                    scale=1.0,
+                )
+            return (b, t0, n_tiles, u_sb, bank_v)
 
-        def finish_by_matrix(b, parts):
-            for t0, n_tiles, u_sb, bank_v in parts:
-                res = work.tile([P, n_tiles, PIX], F32, name="res%d" % n_tiles)
-                for half, sign in enumerate((1.0, -1.0)):
-                    nc.vector.scalar_tensor_tensor(
-                        out=res[:, :, half * P : (half + 1) * P],
-                        in0=bank_v[:, 0 : n_tiles * P].rearrange("p (j c) -> p j c", j=n_tiles),
-                        scalar=sign,
-                        in1=u_sb[:],
-                        op0=ALU.mult,
-                        op1=ALU.add,
-                    )
-                store(b, t0, n_tiles, res)
+        def unfold(b, t0, n_tiles, u_sb, bank_v):
+            res = work.tile([P, n_tiles, PIX], F32, name="res%d" % n_tiles, bufs=5 if n_tiles == PAIR else 3)
+            for half, sign in enumerate((1.0, -1.0)):
+                nc.vector.scalar_tensor_tensor(
+                    out=res[:, :, half * P : (half + 1) * P],
+                    in0=bank_v[:, 0 : n_tiles * P].rearrange("p (j c) -> p j c", j=n_tiles),
+                    scalar=sign,
+                    in1=u_sb[:, 0:n_tiles, :],
+                    op0=ALU.mult,
+                    op1=ALU.add,
+                )
+            store(b, t0, n_tiles, res)
 
+
+        build_matrices(5)
+        regroup_x(0, nc.vector.tensor_copy)
+        build_matrices(3)
+        quantise_x(0)
+        mb_sb = const.tile([P, D_TILES], F32)
+        nc.vector.tensor_copy(out=mb_sb[:], in_=mb_t[:, 0:D_TILES])
+        w_sum = const.tile([P, B], F32)
+        nc.vector.reduce_sum(out=w_sum[:], in_=w_f32[:].rearrange("p (i b) -> p b i", b=B), axis=mybir.AxisListType.X)
+        mb_w = const.tile([P, B, D_TILES], F32)
+        nc.vector.tensor_tensor(
+            out=mb_w[:],
+            in0=mb_sb[:].unsqueeze(1).to_broadcast([P, B, D_TILES]),
+            in1=w_sum[:].unsqueeze(2).to_broadcast([P, B, D_TILES]),
+            op=ALU.mult,
+        )
+        for t in range(D_TILES):
+            transpose_mw(t)
+            if t > 0:
+                quantise_mw(t - 1)
+                build_matrices(3)
+        quantise_mw(D_TILES - 1)
+        build_matrices(len(matrix_steps))
+
+        regroup_x(1, nc.vector.tensor_copy)
+        quantise_x(1)
+        regroup_x(2, nc.vector.tensor_copy)
+        chains = [direct_pair(0, t0) for t0 in range(0, D_TILES, PAIR)]
+        plan_sums(chains[:2])
+        plan_sums(chains[2:])
+        add_terms(2)
+        quantise_x(2)
         folded = dict()
-        chains = dict()
-        parts = dict()
-
-        def multiply(b):
-            if by_matrix(b):
-                folded[b] = multiply_folded(b)
-            if DIRECT_TILES[b] > 0:
-                chains[b] = multiply_direct(b)
-
-        multiply(0)
-        other_terms(matrix_chains[2:])
-        for b in (2, 3):
-            regroup_x(b)
-            quantise_x(b)
-        multiply(1)
-        for b in range(B):
-            if b + 4 < B:
-                regroup_x(b + 4)
+        folded[1] = multiply_folded(1)
+        for b in range(1, B):
             if b + 2 < B:
-                multiply(b + 2)
-            if b + 1 < B and by_matrix(b + 1):
-                parts[b + 1] = apply_matrices(b + 1, folded[b + 1])
-            if by_matrix(b):
-                finish_by_matrix(b, parts[b])
-            if DIRECT_TILES[b] > 0:
-                finish_direct(b, chains[b])
-            if b + 4 < B:
-                quantise_x(b + 4)
+                regroup_x(b + 2, nc.scalar.copy)
+            if b + 1 < B:
+                folded[b + 1] = multiply_folded(b + 1)
+                if DIRECT_TILES[b + 1] > 0:
+                    plan_sums([direct_pair(b + 1, t0) for t0 in range(D_TILES - DIRECT_TILES[b + 1], D_TILES, PAIR)])
+            add_terms(3)
+            if b + 2 < B:
+                quantise_x(b + 2)
+            for t0, n_tiles in tile_groups(0, D_TILES - DIRECT_TILES[b], GROUP):
+                part = apply_matrices(b, folded[b], t0, n_tiles)
+                add_terms(4)
+                unfold(*part)
+        add_terms(len(sum_steps))

@@ -32,8 +32,16 @@ FLOPS = 2 * B * C * C * PIX + 2 * TERMS * B * C * PIX
 DIRECT_TILES = (8, 0, 0, 2, 0, 0)
 
 
+FOLDED_ON_GPSIMD = (1, 4)
+FOLDED_ON_VECTOR = (5,)
+
+
 def by_matrix(b):
     return DIRECT_TILES[b] < D_TILES
+
+
+def negated_in_mx(b):
+    return by_matrix(b) and b not in FOLDED_ON_GPSIMD + FOLDED_ON_VECTOR
 
 
 def tile_groups(first, last, size):
@@ -66,12 +74,16 @@ def tile_graphaugmentation_pa_kernel(tc, x, mw, mb, attn_w, out):
         nc.vector.memset(mb_rows[:], 0.0)
         nc.sync.dma_start(out=mb_rows[0:D_TILES, :], in_=mb.rearrange("(t p) -> t p", p=P))
 
-        load_x(0)
-        for pair in range(D_TILES // 2):
+        def load_mw(t0, n):
             nc.sync.dma_start(
-                out=mw_raw[:, 2 * pair : 2 * pair + 2, :],
-                in_=mw[2 * pair * P : (2 * pair + 2) * P, :].rearrange("(t p) c -> p t c", p=P),
+                out=mw_raw[:, t0 : t0 + n, :],
+                in_=mw[t0 * P : (t0 + n) * P, :].rearrange("(t p) c -> p t c", p=P),
             )
+
+        load_mw(0, 2)
+        load_x(0)
+        for t in range(2, D_TILES, 2):
+            load_mw(t, 2)
         for b in range(1, B):
             load_x(b)
 
@@ -153,8 +165,8 @@ def tile_graphaugmentation_pa_kernel(tc, x, mw, mb, attn_w, out):
 
         x_codes = [keep.tile([P, PASSES, PIX], U32, name="x_codes%d" % b, align_bytes=64) for b in range(B)]
         x_scales = [keep.tile([P, PASSES, PIX], U8, name="x_scales%d" % b, align_bytes=64) for b in range(B)]
-        minus_codes = dict((b, keep.tile([P, PASSES, P], U32, name="minus_codes%d" % b, align_bytes=64)) for b in matrix_images)
-        minus_scales = dict((b, keep.tile([P, PASSES, P], U8, name="minus_scales%d" % b, align_bytes=64)) for b in matrix_images)
+        minus_codes = dict((b, keep.tile([P, PASSES, P], U32, name="minus_codes%d" % b, align_bytes=64)) for b in range(B) if negated_in_mx(b))
+        minus_scales = dict((b, keep.tile([P, PASSES, P], U8, name="minus_scales%d" % b, align_bytes=64)) for b in range(B) if negated_in_mx(b))
         grouped = dict()
         negated = dict()
 
@@ -180,10 +192,10 @@ def tile_graphaugmentation_pa_kernel(tc, x, mw, mb, attn_w, out):
             )
 
         def quantise_x(b):
-            if by_matrix(b):
+            if negated_in_mx(b):
                 negate_x(b)
             quantise(grouped[b], x_codes[b], x_scales[b])
-            if by_matrix(b):
+            if negated_in_mx(b):
                 quantise(negated[b], minus_codes[b], minus_scales[b])
 
         mw_codes = keep.tile([P, PASSES, C], U32, align_bytes=64)
@@ -239,7 +251,7 @@ def tile_graphaugmentation_pa_kernel(tc, x, mw, mb, attn_w, out):
         def store(b, t0, n, res):
             nc.sync.dma_start(
                 out=out[b, t0 * P : (t0 + n) * P].rearrange("(j p) h w -> p j (h w)", p=P),
-                in_=res[:],
+                in_=res[:, :, :],
             )
 
         def shifted(ring, i):
@@ -249,13 +261,13 @@ def tile_graphaugmentation_pa_kernel(tc, x, mw, mb, attn_w, out):
         sum_steps = []
 
         def add_term(chain, i):
-            b, t0, ring, acc, res = chain
+            b, t0, n, ring, acc, res = chain
             if i < TERMS - 1:
                 nc.vector.scalar_tensor_tensor(
-                    out=acc[:], in0=shifted(ring, i), scalar=weight(i, b), in1=acc[:], op0=ALU.mult, op1=ALU.add
+                    out=acc[:, :, :, :], in0=shifted(ring, i), scalar=weight(i, b), in1=acc[:, :, :, :], op0=ALU.mult, op1=ALU.add
                 )
                 return
-            for j in range(PAIR):
+            for j in range(n):
                 nc.vector.scalar_tensor_tensor(
                     out=res[:, j, :].rearrange("p (h w) -> p h w", w=W),
                     in0=shifted(ring, i)[:, :, j, :],
@@ -264,16 +276,17 @@ def tile_graphaugmentation_pa_kernel(tc, x, mw, mb, attn_w, out):
                     op0=ALU.mult,
                     op1=ALU.add,
                 )
-            store(b, t0, PAIR, res)
+            store(b, t0, n, res)
 
         def direct_pair(b, t0):
             ring = work.tile([P, H + 2 * REACH, PAIR, 2 * W], F32, name="ring", bufs=5)
             bank = psum.tile([P, BANK], F32, tag="bank")
-            for j in range(PAIR):
-                t = t0 + j
-                channels = slice(t * P, (t + 1) * P)
-                acc = bank[:, j * PIX : (j + 1) * PIX]
+            halves = [bank[:, j * PIX : (j + 1) * PIX] for j in range(PAIR)]
+            for j, acc in enumerate(halves):
+                channels = slice((t0 + j) * P, (t0 + j + 1) * P)
                 mx_group(acc, [(mw_part(g, channels), x_part(b, g, slice(0, PIX))) for g in range(PASSES)])
+            for j, acc in enumerate(halves):
+                t = t0 + j
                 for ring_row, image_row, n in [(REACH, 0, H), (0, H - REACH, REACH), (REACH + H, 0, REACH)]:
                     nc.scalar.activation(
                         out=ring[:, ring_row : ring_row + n, j, :].rearrange("p r (c w) -> p r c w", c=2),
@@ -285,20 +298,28 @@ def tile_graphaugmentation_pa_kernel(tc, x, mw, mb, attn_w, out):
                         bias=mb_sb[:, t : t + 1],
                         scale=1.0,
                     )
-            first = work.tile([P, H, PAIR, W], F32, name="acc", bufs=5)
-            nc.scalar.activation(out=first[:], in_=shifted(ring, 0), func=ACT.Copy, scale=weight(0, b))
+            acc = work.tile([P, H, PAIR, W], F32, name="acc", bufs=5)
+            nc.scalar.activation(out=acc[:], in_=shifted(ring, 0), func=ACT.Copy, scale=weight(0, b))
             res = work.tile([P, PAIR, PIX], F32, name="res2", bufs=5)
-            return (b, t0, ring, first, res)
+            return (b, t0, PAIR, ring, acc, res)
+
+        def split(chain):
+            b, t0, n, ring, acc, res = chain
+            return [
+                (b, t0 + j, 1, ring[:, :, j : j + 1, :], acc[:, :, j : j + 1, :], res[:, j : j + 1, :]) for j in range(n)
+            ]
 
         def plan_sums(chains):
             for i in range(1, TERMS):
                 for chain in chains:
                     sum_steps.append((chain, i))
 
-        def add_terms(steps):
-            for k in range(min(steps, len(sum_steps))):
-                add_term(*sum_steps[0])
+        def add_terms(tiles):
+            while tiles > 0 and sum_steps:
+                chain, i = sum_steps[0]
+                add_term(chain, i)
                 sum_steps.remove(sum_steps[0])
+                tiles -= chain[2]
 
         def multiply_folded(b):
             folded = work.tile([P, 2, C], F32, name="folded", bufs=2)
@@ -314,6 +335,49 @@ def tile_graphaugmentation_pa_kernel(tc, x, mw, mb, attn_w, out):
                     mx_group(bank[:, 0 : n_tiles * P], lower + upper)
                     nc.scalar.copy(out=folded[:, sign, channels], in_=bank[:, 0 : n_tiles * P])
             return folded
+
+        def multiply_halves(b):
+            halves = work.tile([P, 2, C], F32, name="halves", bufs=2)
+            folded = work.tile([P, 2, C], F32, name="folded", bufs=2)
+            for t0, n_tiles in tile_groups(0, D_TILES - DIRECT_TILES[b], GROUP):
+                channels = slice(t0 * P, (t0 + n_tiles) * P)
+                for half in range(2):
+                    bank = psum.tile([P, BANK], F32, tag="bank")
+                    mx_group(
+                        bank[:, 0 : n_tiles * P],
+                        [(x_part(b, g, slice(half * P, (half + 1) * P)), mw_part(g, channels)) for g in range(PASSES)],
+                    )
+                    nc.scalar.copy(out=halves[:, half, channels], in_=bank[:, 0 : n_tiles * P])
+                for sign, op in enumerate((ALU.add, ALU.subtract)):
+                    nc.gpsimd.tensor_tensor(
+                        out=folded[:, sign, channels], in0=halves[:, 0, channels], in1=halves[:, 1, channels], op=op
+                    )
+            return folded
+
+        def multiply_for_vector(b):
+            folded = work.tile([P, 2, C], F32, name="folded", bufs=2)
+            for t0, n_tiles in tile_groups(0, D_TILES - DIRECT_TILES[b], GROUP):
+                channels = slice(t0 * P, (t0 + n_tiles) * P)
+                banks = []
+                for half in (1, 0):
+                    bank = psum.tile([P, BANK], F32, tag="bank")
+                    mx_group(
+                        bank[:, 0 : n_tiles * P],
+                        [(x_part(b, g, slice(half * P, (half + 1) * P)), mw_part(g, channels)) for g in range(PASSES)],
+                    )
+                    banks.append(bank)
+                upper = work.tile([P, BANK], F32, name="upper", bufs=2)
+                nc.scalar.copy(out=upper[:, 0 : n_tiles * P], in_=banks[0][:, 0 : n_tiles * P])
+                for sign, op in enumerate((ALU.add, ALU.subtract)):
+                    nc.vector.tensor_tensor(
+                        out=folded[:, sign, channels], in0=banks[1][:, 0 : n_tiles * P], in1=upper[:, 0 : n_tiles * P], op=op
+                    )
+            return folded
+
+        def multiply(b):
+            if b in FOLDED_ON_GPSIMD:
+                return multiply_halves(b)
+            return multiply_for_vector(b) if b in FOLDED_ON_VECTOR else multiply_folded(b)
 
         def apply_matrices(b, folded, t0, n_tiles):
             bank_u = psum.tile([P, BANK], F32, tag="bank")
@@ -354,14 +418,14 @@ def tile_graphaugmentation_pa_kernel(tc, x, mw, mb, attn_w, out):
             store(b, t0, n_tiles, res)
 
 
-        build_matrices(5)
+        build_matrices(12)
         regroup_x(0, nc.vector.tensor_copy)
-        build_matrices(3)
-        quantise_x(0)
+        build_matrices(1)
         mb_sb = const.tile([P, D_TILES], F32)
         nc.vector.tensor_copy(out=mb_sb[:], in_=mb_t[:, 0:D_TILES])
         w_sum = const.tile([P, B], F32)
         nc.vector.reduce_sum(out=w_sum[:], in_=w_f32[:].rearrange("p (i b) -> p b i", b=B), axis=mybir.AxisListType.X)
+        quantise_x(0)
         mb_w = const.tile([P, B, D_TILES], F32)
         nc.vector.tensor_tensor(
             out=mb_w[:],
@@ -373,32 +437,39 @@ def tile_graphaugmentation_pa_kernel(tc, x, mw, mb, attn_w, out):
             transpose_mw(t)
             if t > 0:
                 quantise_mw(t - 1)
-                build_matrices(3)
-        quantise_mw(D_TILES - 1)
-        build_matrices(len(matrix_steps))
-
         regroup_x(1, nc.vector.tensor_copy)
+        quantise_mw(D_TILES - 1)
         quantise_x(1)
-        regroup_x(2, nc.vector.tensor_copy)
-        chains = [direct_pair(0, t0) for t0 in range(0, D_TILES, PAIR)]
-        plan_sums(chains[:2])
-        plan_sums(chains[2:])
-        add_terms(2)
-        quantise_x(2)
+
         folded = dict()
-        folded[1] = multiply_folded(1)
+        chains = [direct_pair(0, 0)]
+        folded[1] = multiply(1)
+        chains.append(direct_pair(0, 2))
+        regroup_x(2, nc.vector.tensor_copy)
+        build_matrices(4)
+        quantise_x(2)
+        build_matrices(len(matrix_steps))
+        regroup_x(3, nc.scalar.copy)
+        folded[2] = multiply(2)
+        plan_sums(chains)
+        chains = [direct_pair(0, 4)]
+        add_terms(8)
+        quantise_x(3)
+        add_terms(20)
         for b in range(1, B):
-            if b + 2 < B:
-                regroup_x(b + 2, nc.scalar.copy)
-            if b + 1 < B:
-                folded[b + 1] = multiply_folded(b + 1)
-                if DIRECT_TILES[b + 1] > 0:
-                    plan_sums([direct_pair(b + 1, t0) for t0 in range(D_TILES - DIRECT_TILES[b + 1], D_TILES, PAIR)])
-            add_terms(3)
-            if b + 2 < B:
-                quantise_x(b + 2)
-            for t0, n_tiles in tile_groups(0, D_TILES - DIRECT_TILES[b], GROUP):
+            if b + 3 < B:
+                regroup_x(b + 3, nc.scalar.copy)
+            if b > 1 and b + 1 < B:
+                folded[b + 1] = multiply(b + 1)
+            if b == 1:
+                plan_sums(chains + [direct_pair(0, 6)])
+                add_terms(4)
+            if b == 2:
+                plan_sums(split(direct_pair(3, 6)))
+            for g, (t0, n_tiles) in enumerate(tile_groups(0, D_TILES - DIRECT_TILES[b], GROUP)):
                 part = apply_matrices(b, folded[b], t0, n_tiles)
                 add_terms(4)
                 unfold(*part)
-        add_terms(len(sum_steps))
+                if g == 0 and b + 3 < B:
+                    quantise_x(b + 3)
+        add_terms(70)

@@ -32,7 +32,7 @@ FLOPS = 2 * B * C * C * PIX + 2 * TERMS * B * C * PIX
 DIRECT_TILES = (8, 0, 0, 2, 0, 0)
 
 
-FOLDED_ON_GPSIMD = (1, 4)
+FOLDED_ON_GPSIMD = ()
 FOLDED_ON_VECTOR = (5,)
 
 
@@ -153,14 +153,16 @@ def tile_graphaugmentation_pa_kernel(tc, x, mw, mb, attn_w, out):
                 op0=ALU.mult,
                 op1=ALU.add,
             )
-            if i == TERMS - 1:
-                nc.gpsimd.tensor_tensor(out=matrix[b][:, 1, :], in0=matrix[b][:, 0, :], in1=edge_sign[:], op=ALU.mult)
 
-        matrix_steps = [(b, i) for i in range(1, TERMS) for b in matrix_images]
+        matrix_steps = [(b, i) for i in range(1, TERMS + 1) for b in matrix_images]
 
         def build_matrices(steps):
             for k in range(min(steps, len(matrix_steps))):
-                matrix_term(*matrix_steps[0])
+                b, i = matrix_steps[0]
+                if i < TERMS:
+                    matrix_term(b, i)
+                else:
+                    nc.vector.tensor_tensor(out=matrix[b][:, 1, :], in0=matrix[b][:, 0, :], in1=edge_sign[:], op=ALU.mult)
                 matrix_steps.remove(matrix_steps[0])
 
         x_codes = [keep.tile([P, PASSES, PIX], U32, name="x_codes%d" % b, align_bytes=64) for b in range(B)]

@@ -84,34 +84,30 @@ def tile_graphaugmentation_pa_kernel(tc, x, mw, mb, attn_w, out):
         load_x(0)
         for t in range(2, D_TILES, 2):
             load_mw(t, 2)
-        for b in range(1, B):
-            load_x(b)
+        load_x(1)
+        load_x(2)
 
         ident = const.tile([P, P], F32)
         make_identity(nc, ident[:])
 
-        half_ring = const.tile([P, HALF_ROWS + 2 * REACH, 2 * W], F32)
-        sign_ring = const.tile([P, HALF_ROWS + 2 * REACH, 2 * W], F32)
-        for ring_row, image_row, n, beyond in [
-            (0, HALF_ROWS - REACH, REACH, True),
-            (REACH, 0, HALF_ROWS, False),
-            (REACH + HALF_ROWS, 0, REACH, True),
-        ]:
-            rows = (
-                ident[:, image_row * W : (image_row + n) * W]
-                .rearrange("p (r w) -> p r w", w=W)
-                .unsqueeze(2)
-                .to_broadcast([P, n, 2, W])
+        def weight(i, b):
+            return w_f32[:, i * B + b : i * B + b + 1]
+
+        STRIP = 2 * HALF_ROWS * W
+        strips = const.tile([W, len(matrix_images), 2 * STRIP], F32)
+        nc.vector.memset(strips[:], 0.0)
+        unit = const.tile([W, 2, 4, 2 * W], F32)
+        nc.vector.tensor_scalar_mul(
+            out=unit[:].rearrange("q k s (c w) -> q (k s c) w", c=2),
+            in0=ident[0:W, 0:W].unsqueeze(1).to_broadcast([W, 2 * 4 * 2, W]),
+            scalar1=0.5,
+        )
+        for k, over_the_edge in [(0, 3), (1, 2)]:
+            nc.vector.tensor_scalar_mul(
+                out=unit[:, k, over_the_edge, :].rearrange("q (c w) -> q c w", c=2),
+                in0=ident[0:W, 0:W].unsqueeze(1).to_broadcast([W, 2, W]),
+                scalar1=-0.5,
             )
-
-            def ring_rows(ring):
-                return ring[:, ring_row : ring_row + n, :].rearrange("p r (c w) -> p r c w", c=2)
-
-            nc.vector.tensor_scalar_mul(out=ring_rows(half_ring), in0=rows, scalar1=0.5)
-            nc.gpsimd.tensor_scalar(
-                out=ring_rows(sign_ring), in0=rows, scalar1=-1.0 if beyond else 1.0, scalar2=0.0, op0=ALU.mult, op1=ALU.add
-            )
-
         w_f32 = const.tile([P, TERMS * B], F32)
         nc.vector.tensor_copy(out=w_f32[:], in_=w_bf[:])
 
@@ -119,51 +115,29 @@ def tile_graphaugmentation_pa_kernel(tc, x, mw, mb, attn_w, out):
         nc.vector.tensor_copy(out=mb_rows_f32[:], in_=mb_rows[:])
         mb_t = psum.tile([P, BANK], F32, tag="bank")
         nc.tensor.transpose(mb_t[:, 0:P], mb_rows_f32[:], ident[:])
-
-        def weight(i, b):
-            return w_f32[:, i * B + b : i * B + b + 1]
-
-        def half_shifted(ring, i):
-            dy, dx = OFFSETS[i]
-            return ring[:, REACH - dy : REACH - dy + HALF_ROWS, (-dx) % W : (-dx) % W + W]
-
-        def image_rows(matrix):
-            return matrix.rearrange("p (h w) -> p h w", w=W)
-
-        edge_sign = const.tile([P, P], F32)
-        nc.gpsimd.tensor_tensor(
-            out=image_rows(edge_sign[:]), in0=half_shifted(sign_ring, 0), in1=half_shifted(sign_ring, 1), op=ALU.add
-        )
-        for i in range(2, TERMS):
-            nc.gpsimd.tensor_tensor(
-                out=image_rows(edge_sign[:]), in0=image_rows(edge_sign[:]), in1=half_shifted(sign_ring, i), op=ALU.add
-            )
-        matrix = dict((b, const.tile([P, 2, P], F32, name="matrix%d" % b)) for b in matrix_images)
-        for b in matrix_images:
-            nc.scalar.activation(
-                out=image_rows(matrix[b][:, 0, :]), in_=half_shifted(half_ring, 0), func=ACT.Copy, scale=weight(0, b)
-            )
-
-        def matrix_term(b, i):
-            nc.vector.scalar_tensor_tensor(
-                out=image_rows(matrix[b][:, 0, :]),
-                in0=half_shifted(half_ring, i),
-                scalar=weight(i, b),
-                in1=image_rows(matrix[b][:, 0, :]),
-                op0=ALU.mult,
-                op1=ALU.add,
-            )
-
-        matrix_steps = [(b, i) for i in range(1, TERMS + 1) for b in matrix_images]
-
-        def build_matrices(steps):
-            for k in range(min(steps, len(matrix_steps))):
-                b, i = matrix_steps[0]
-                if i < TERMS:
-                    matrix_term(b, i)
+        filled = set()
+        for i, (dy, dx) in enumerate(OFFSETS):
+            for n, b in enumerate(matrix_images):
+                row = (dy % HALF_ROWS) * W
+                place = strips[:, n, :].rearrange("q (s r) -> q s r", s=4)[:, :, row : row + W]
+                values = unit[:, 1 if dy > 0 else 0, :, (-dx) % W : (-dx) % W + W]
+                w_16 = w_f32[0:W, i * B + b : i * B + b + 1]
+                if (row, n) in filled:
+                    nc.vector.scalar_tensor_tensor(out=place, in0=values, scalar=w_16, in1=place, op0=ALU.mult, op1=ALU.add)
                 else:
-                    nc.vector.tensor_tensor(out=matrix[b][:, 1, :], in0=matrix[b][:, 0, :], in1=edge_sign[:], op=ALU.mult)
-                matrix_steps.remove(matrix_steps[0])
+                    nc.vector.tensor_scalar_mul(out=place, in0=values, scalar1=w_16)
+                filled.add((row, n))
+        matrices = const.tile([P, 2 * len(matrix_images), P], F32)
+        parked = out[B - 1, 0 : W * 2 * len(matrix_images)].rearrange("(w m) h c -> w m (h c)", w=W)
+
+        def spread_matrices():
+            nc.sync.dma_start(out=parked, in_=strips[:].rearrange("q n (s r) -> q (n s) r", s=2))
+            for h in range(HALF_ROWS):
+                start = (HALF_ROWS - h) * W
+                nc.sync.dma_start(out=matrices[h * W : (h + 1) * W, :, :], in_=parked[:, :, start : start + P])
+
+        def matrix(b, sign):
+            return matrices[:, 2 * matrix_images.index(b) + sign, :]
 
         x_codes = [keep.tile([P, PASSES, PIX], U32, name="x_codes%d" % b, align_bytes=64) for b in range(B)]
         x_scales = [keep.tile([P, PASSES, PIX], U8, name="x_scales%d" % b, align_bytes=64) for b in range(B)]
@@ -280,15 +254,21 @@ def tile_graphaugmentation_pa_kernel(tc, x, mw, mb, attn_w, out):
                 )
             store(b, t0, n, res)
 
-        def direct_pair(b, t0):
-            ring = work.tile([P, H + 2 * REACH, PAIR, 2 * W], F32, name="ring", bufs=5)
+        def multiply_direct(b, t0):
             bank = psum.tile([P, BANK], F32, tag="bank")
-            halves = [bank[:, j * PIX : (j + 1) * PIX] for j in range(PAIR)]
-            for j, acc in enumerate(halves):
+            for j in range(PAIR):
                 channels = slice((t0 + j) * P, (t0 + j + 1) * P)
-                mx_group(acc, [(mw_part(g, channels), x_part(b, g, slice(0, PIX))) for g in range(PASSES)])
-            for j, acc in enumerate(halves):
+                mx_group(
+                    bank[:, j * PIX : (j + 1) * PIX],
+                    [(mw_part(g, channels), x_part(b, g, slice(0, PIX))) for g in range(PASSES)],
+                )
+            return (b, t0, bank)
+
+        def start_sum(b, t0, bank):
+            ring = work.tile([P, H + 2 * REACH, PAIR, 2 * W], F32, name="ring", bufs=5)
+            for j in range(PAIR):
                 t = t0 + j
+                acc = bank[:, j * PIX : (j + 1) * PIX]
                 for ring_row, image_row, n in [(REACH, 0, H), (0, H - REACH, REACH), (REACH + H, 0, REACH)]:
                     nc.scalar.activation(
                         out=ring[:, ring_row : ring_row + n, j, :].rearrange("p r (c w) -> p r c w", c=2),
@@ -390,7 +370,7 @@ def tile_graphaugmentation_pa_kernel(tc, x, mw, mb, attn_w, out):
                     nc.tensor.matmul(
                         out=bank[:, j * P : (j + 1) * P],
                         lhsT=folded[:, sign, t * P : (t + 1) * P],
-                        rhs=matrix[b][:, sign, :],
+                        rhs=matrix(b, sign),
                         start=True,
                         stop=True,
                     )
@@ -420,9 +400,7 @@ def tile_graphaugmentation_pa_kernel(tc, x, mw, mb, attn_w, out):
             store(b, t0, n_tiles, res)
 
 
-        build_matrices(12)
         regroup_x(0, nc.vector.tensor_copy)
-        build_matrices(1)
         mb_sb = const.tile([P, D_TILES], F32)
         nc.vector.tensor_copy(out=mb_sb[:], in_=mb_t[:, 0:D_TILES])
         w_sum = const.tile([P, B], F32)
@@ -435,6 +413,9 @@ def tile_graphaugmentation_pa_kernel(tc, x, mw, mb, attn_w, out):
             in1=w_sum[:].unsqueeze(2).to_broadcast([P, B, D_TILES]),
             op=ALU.mult,
         )
+        spread_matrices()
+        for b in range(3, B):
+            load_x(b)
         for t in range(D_TILES):
             transpose_mw(t)
             if t > 0:
@@ -443,19 +424,18 @@ def tile_graphaugmentation_pa_kernel(tc, x, mw, mb, attn_w, out):
         quantise_mw(D_TILES - 1)
         quantise_x(1)
 
+        products = [multiply_direct(0, t0) for t0 in range(0, D_TILES, PAIR)]
+        plan_sums([start_sum(*product) for product in products[:2]])
         folded = dict()
-        chains = [direct_pair(0, 0)]
         folded[1] = multiply(1)
-        chains.append(direct_pair(0, 2))
+        plan_sums([start_sum(*product) for product in products[2:]])
         regroup_x(2, nc.vector.tensor_copy)
-        build_matrices(4)
+        add_terms(2)
         quantise_x(2)
-        build_matrices(len(matrix_steps))
-        regroup_x(3, nc.scalar.copy)
         folded[2] = multiply(2)
-        plan_sums(chains)
-        chains = [direct_pair(0, 4)]
         add_terms(8)
+        regroup_x(3, nc.vector.tensor_copy)
+        add_terms(2)
         quantise_x(3)
         add_terms(20)
         for b in range(1, B):
@@ -463,11 +443,8 @@ def tile_graphaugmentation_pa_kernel(tc, x, mw, mb, attn_w, out):
                 regroup_x(b + 3, nc.scalar.copy)
             if b > 1 and b + 1 < B:
                 folded[b + 1] = multiply(b + 1)
-            if b == 1:
-                plan_sums(chains + [direct_pair(0, 6)])
-                add_terms(4)
             if b == 2:
-                plan_sums(split(direct_pair(3, 6)))
+                plan_sums(split(start_sum(*multiply_direct(3, 6))))
             for g, (t0, n_tiles) in enumerate(tile_groups(0, D_TILES - DIRECT_TILES[b], GROUP)):
                 part = apply_matrices(b, folded[b], t0, n_tiles)
                 add_terms(4)

@@ -32,16 +32,8 @@ FLOPS = 2 * B * C * C * PIX + 2 * TERMS * B * C * PIX
 DIRECT_TILES = (8, 0, 0, 2, 0, 0)
 
 
-FOLDED_ON_GPSIMD = ()
-FOLDED_ON_VECTOR = (5,)
-
-
 def by_matrix(b):
     return DIRECT_TILES[b] < D_TILES
-
-
-def negated_in_mx(b):
-    return by_matrix(b) and b not in FOLDED_ON_GPSIMD + FOLDED_ON_VECTOR
 
 
 def tile_groups(first, last, size):
@@ -95,7 +87,9 @@ def tile_graphaugmentation_pa_kernel(tc, x, mw, mb, attn_w, out):
 
         STRIP = 2 * HALF_ROWS * W
         strips = const.tile([W, len(matrix_images), 2 * STRIP], F32)
-        nc.vector.memset(strips[:], 0.0)
+        strip_rows = strips[:].rearrange("q n (s r) -> q (n s) r", r=HALF_ROWS * W)
+        nc.vector.memset(strip_rows[:, :, 0 : 2 * W], 0.0)
+        nc.vector.memset(strip_rows[:, :, 7 * W : 8 * W], 0.0)
         unit = const.tile([W, 2, 4, 2 * W], F32)
         nc.vector.tensor_scalar_mul(
             out=unit[:].rearrange("q k s (c w) -> q (k s c) w", c=2),
@@ -141,10 +135,7 @@ def tile_graphaugmentation_pa_kernel(tc, x, mw, mb, attn_w, out):
 
         x_codes = [keep.tile([P, PASSES, PIX], U32, name="x_codes%d" % b, align_bytes=64) for b in range(B)]
         x_scales = [keep.tile([P, PASSES, PIX], U8, name="x_scales%d" % b, align_bytes=64) for b in range(B)]
-        minus_codes = dict((b, keep.tile([P, PASSES, P], U32, name="minus_codes%d" % b, align_bytes=64)) for b in range(B) if negated_in_mx(b))
-        minus_scales = dict((b, keep.tile([P, PASSES, P], U8, name="minus_scales%d" % b, align_bytes=64)) for b in range(B) if negated_in_mx(b))
         grouped = dict()
-        negated = dict()
 
         def regroup_x(b, copy):
             x_grp = stage.tile([P, PASSES, PIX * PACK], BF16, name="x_grp", align_bytes=64)
@@ -155,24 +146,12 @@ def tile_graphaugmentation_pa_kernel(tc, x, mw, mb, attn_w, out):
                 )
             grouped[b] = x_grp
 
-        def negate_x(b):
-            minus_grp = stage.tile([P, PASSES, P * PACK], BF16, name="minus_grp", align_bytes=64)
-            nc.vector.tensor_scalar_mul(out=minus_grp[:], in0=grouped[b][:, :, P * PACK : 2 * P * PACK], scalar1=-1.0)
-            negated[b] = minus_grp
-
-        def quantise(values, codes, scales):
-            nc.vector.quantize_mx(
-                out=codes[:].rearrange("q g c -> q (g c)").bitcast(FP8X4),
-                scales=scales[:].rearrange("q g c -> q (g c)"),
-                in_=values[:].rearrange("q g c -> q (g c)"),
-            )
-
         def quantise_x(b):
-            if negated_in_mx(b):
-                negate_x(b)
-            quantise(grouped[b], x_codes[b], x_scales[b])
-            if negated_in_mx(b):
-                quantise(negated[b], minus_codes[b], minus_scales[b])
+            nc.vector.quantize_mx(
+                out=x_codes[b][:].rearrange("q g c -> q (g c)").bitcast(FP8X4),
+                scales=x_scales[b][:].rearrange("q g c -> q (g c)"),
+                in_=grouped[b][:].rearrange("q g c -> q (g c)"),
+            )
 
         mw_codes = keep.tile([P, PASSES, C], U32, align_bytes=64)
         mw_scales = keep.tile([P, PASSES, C], U8, align_bytes=64)
@@ -208,9 +187,6 @@ def tile_graphaugmentation_pa_kernel(tc, x, mw, mb, attn_w, out):
 
         def x_part(b, g, pixels):
             return (x_codes[b][:, g, pixels], x_scales[b][:, g, pixels])
-
-        def minus_part(b, g):
-            return (minus_codes[b][:, g, :], minus_scales[b][:, g, :])
 
         def mx_group(acc, pairs):
             for k, (still, moving) in enumerate(pairs):
@@ -303,63 +279,25 @@ def tile_graphaugmentation_pa_kernel(tc, x, mw, mb, attn_w, out):
                 sum_steps.remove(sum_steps[0])
                 tiles -= chain[2]
 
-        def multiply_folded(b):
-            folded = work.tile([P, 2, C], F32, name="folded", bufs=2)
-            for sign in range(2):
-                for t0, n_tiles in tile_groups(0, D_TILES - DIRECT_TILES[b], GROUP):
-                    channels = slice(t0 * P, (t0 + n_tiles) * P)
-                    bank = psum.tile([P, BANK], F32, tag="bank")
-                    lower = [(x_part(b, g, slice(0, P)), mw_part(g, channels)) for g in range(PASSES)]
-                    upper = [
-                        (x_part(b, g, slice(P, 2 * P)) if sign == 0 else minus_part(b, g), mw_part(g, channels))
-                        for g in range(PASSES)
-                    ]
-                    mx_group(bank[:, 0 : n_tiles * P], lower + upper)
-                    nc.scalar.copy(out=folded[:, sign, channels], in_=bank[:, 0 : n_tiles * P])
-            return folded
-
-        def multiply_halves(b):
-            halves = work.tile([P, 2, C], F32, name="halves", bufs=2)
-            folded = work.tile([P, 2, C], F32, name="folded", bufs=2)
-            for t0, n_tiles in tile_groups(0, D_TILES - DIRECT_TILES[b], GROUP):
-                channels = slice(t0 * P, (t0 + n_tiles) * P)
-                for half in range(2):
-                    bank = psum.tile([P, BANK], F32, tag="bank")
-                    mx_group(
-                        bank[:, 0 : n_tiles * P],
-                        [(x_part(b, g, slice(half * P, (half + 1) * P)), mw_part(g, channels)) for g in range(PASSES)],
-                    )
-                    nc.scalar.copy(out=halves[:, half, channels], in_=bank[:, 0 : n_tiles * P])
-                for sign, op in enumerate((ALU.add, ALU.subtract)):
-                    nc.gpsimd.tensor_tensor(
-                        out=folded[:, sign, channels], in0=halves[:, 0, channels], in1=halves[:, 1, channels], op=op
-                    )
-            return folded
-
-        def multiply_for_vector(b):
-            folded = work.tile([P, 2, C], F32, name="folded", bufs=2)
-            for t0, n_tiles in tile_groups(0, D_TILES - DIRECT_TILES[b], GROUP):
-                channels = slice(t0 * P, (t0 + n_tiles) * P)
-                banks = []
-                for half in (1, 0):
-                    bank = psum.tile([P, BANK], F32, tag="bank")
-                    mx_group(
-                        bank[:, 0 : n_tiles * P],
-                        [(x_part(b, g, slice(half * P, (half + 1) * P)), mw_part(g, channels)) for g in range(PASSES)],
-                    )
-                    banks.append(bank)
-                upper = work.tile([P, BANK], F32, name="upper", bufs=2)
-                nc.scalar.copy(out=upper[:, 0 : n_tiles * P], in_=banks[0][:, 0 : n_tiles * P])
-                for sign, op in enumerate((ALU.add, ALU.subtract)):
-                    nc.vector.tensor_tensor(
-                        out=folded[:, sign, channels], in0=banks[1][:, 0 : n_tiles * P], in1=upper[:, 0 : n_tiles * P], op=op
-                    )
-            return folded
-
         def multiply(b):
-            if b in FOLDED_ON_GPSIMD:
-                return multiply_halves(b)
-            return multiply_for_vector(b) if b in FOLDED_ON_VECTOR else multiply_folded(b)
+            folded = work.tile([P, 2, C], F32, name="folded", bufs=2)
+            parts = []
+            for t0, n_tiles in tile_groups(0, D_TILES - DIRECT_TILES[b], GROUP):
+                channels = slice(t0 * P, (t0 + n_tiles) * P)
+                lower = [(x_part(b, g, slice(0, P)), mw_part(g, channels)) for g in range(PASSES)]
+                upper = [(x_part(b, g, slice(P, 2 * P)), mw_part(g, channels)) for g in range(PASSES)]
+                bank_sum = psum.tile([P, BANK], F32, tag="bank")
+                mx_group(bank_sum[:, 0 : n_tiles * P], lower + upper)
+                nc.scalar.copy(out=folded[:, 0, channels], in_=bank_sum[:, 0 : n_tiles * P])
+                bank_lo = psum.tile([P, BANK], F32, tag="bank")
+                mx_group(bank_lo[:, 0 : n_tiles * P], lower)
+                parts.append((folded, channels, bank_lo[:, 0 : n_tiles * P]))
+            return parts
+
+        def subtract(folded, channels, lo):
+            nc.vector.scalar_tensor_tensor(
+                out=folded[:, 1, channels], in0=lo, scalar=2.0, in1=folded[:, 0, channels], op0=ALU.mult, op1=ALU.subtract
+            )
 
         def apply_matrices(b, folded, t0, n_tiles):
             bank_u = psum.tile([P, BANK], F32, tag="bank")
@@ -387,7 +325,7 @@ def tile_graphaugmentation_pa_kernel(tc, x, mw, mb, attn_w, out):
             return (b, t0, n_tiles, u_sb, bank_v)
 
         def unfold(b, t0, n_tiles, u_sb, bank_v):
-            res = work.tile([P, n_tiles, PIX], F32, name="res%d" % n_tiles, bufs=5 if n_tiles == PAIR else 3)
+            res = work.tile([P, n_tiles, PIX], F32, name="res_folded%d" % n_tiles, bufs=4 if n_tiles == PAIR else 3)
             for half, sign in enumerate((1.0, -1.0)):
                 nc.vector.scalar_tensor_tensor(
                     out=res[:, :, half * P : (half + 1) * P],
@@ -426,18 +364,26 @@ def tile_graphaugmentation_pa_kernel(tc, x, mw, mb, attn_w, out):
 
         products = [multiply_direct(0, t0) for t0 in range(0, D_TILES, PAIR)]
         plan_sums([start_sum(*product) for product in products[:2]])
+
         folded = dict()
         folded[1] = multiply(1)
-        plan_sums([start_sum(*product) for product in products[2:]])
         regroup_x(2, nc.vector.tensor_copy)
+        plan_sums([start_sum(*product) for product in products[2:]])
         add_terms(2)
         quantise_x(2)
+
+        for part in folded[1]:
+            add_terms(4)
+            subtract(*part)
         folded[2] = multiply(2)
-        add_terms(8)
+        add_terms(4)
         regroup_x(3, nc.vector.tensor_copy)
         add_terms(2)
         quantise_x(3)
-        add_terms(20)
+        for part in folded[2]:
+            add_terms(2)
+            subtract(*part)
+        add_terms(4)
         for b in range(1, B):
             if b + 3 < B:
                 regroup_x(b + 3, nc.scalar.copy)
@@ -445,9 +391,11 @@ def tile_graphaugmentation_pa_kernel(tc, x, mw, mb, attn_w, out):
                 folded[b + 1] = multiply(b + 1)
             if b == 2:
                 plan_sums(split(start_sum(*multiply_direct(3, 6))))
-            for g, (t0, n_tiles) in enumerate(tile_groups(0, D_TILES - DIRECT_TILES[b], GROUP)):
-                part = apply_matrices(b, folded[b], t0, n_tiles)
-                add_terms(4)
+            for g, (t0, n_tiles) in enumerate(tile_groups(0, D_TILES - DIRECT_TILES[b], GROUP if b + 1 < B else PAIR)):
+                if b > 1 and b + 1 < B:
+                    subtract(*folded[b + 1][g])
+                part = apply_matrices(b, folded[b][0][0], t0, n_tiles)
+                add_terms(8 if b == 4 and g == 0 else 4)
                 unfold(*part)
                 if g == 0 and b + 3 < B:
                     quantise_x(b + 3)

@@ -24,6 +24,8 @@ D_TILES = C // P
 OFFSETS = [(-4, -4), (-4, -1), (-4, 2), (-3, 4), (-2, -3), (2, 3), (3, -2), (4, 4)]
 TERMS = len(OFFSETS)
 REACH = 4
+W_ROW = D_TILES
+SLOTS = P // W
 GROUP = 4
 PAIR = 2
 
@@ -60,11 +62,10 @@ def tile_graphaugmentation_pa_kernel(tc, x, mw, mb, attn_w, out):
                 in_=x[b].rearrange("(g q t) h w -> q g (t h w)", q=P, t=PACK),
             )
 
-        w_bf = const.tile([P, TERMS * B], BF16)
-        nc.sync.dma_start(out=w_bf[:], in_=attn_w.rearrange("i b -> (i b)").partition_broadcast(P))
-        mb_rows = const.tile([P, P], BF16)
-        nc.vector.memset(mb_rows[:], 0.0)
-        nc.sync.dma_start(out=mb_rows[0:D_TILES, :], in_=mb.rearrange("(t p) -> t p", p=P))
+        small_rows = const.tile([P, P], BF16)
+        nc.vector.memset(small_rows[:], 0.0)
+        nc.scalar.dma_start(out=small_rows[W_ROW : W_ROW + 1, 0 : TERMS * B], in_=attn_w.rearrange("(o i) b -> o (i b)", o=1))
+        nc.scalar.dma_start(out=small_rows[0:D_TILES, :], in_=mb.rearrange("(t p) -> t p", p=P))
 
         def load_mw(t0, n):
             nc.sync.dma_start(
@@ -72,12 +73,13 @@ def tile_graphaugmentation_pa_kernel(tc, x, mw, mb, attn_w, out):
                 in_=mw[t0 * P : (t0 + n) * P, :].rearrange("(t p) c -> p t c", p=P),
             )
 
-        load_mw(0, 2)
         load_x(0)
-        for t in range(2, D_TILES, 2):
-            load_mw(t, 2)
+        load_mw(0, 1)
+        load_mw(1, 1)
+        load_mw(2, 2)
         load_x(1)
-        load_x(2)
+        load_mw(4, 2)
+        load_mw(6, 2)
 
         ident = const.tile([P, P], F32)
         make_identity(nc, ident[:])
@@ -86,49 +88,78 @@ def tile_graphaugmentation_pa_kernel(tc, x, mw, mb, attn_w, out):
             return w_f32[:, i * B + b : i * B + b + 1]
 
         STRIP = 2 * HALF_ROWS * W
-        strips = const.tile([W, len(matrix_images), 2 * STRIP], F32)
-        strip_rows = strips[:].rearrange("q n (s r) -> q (n s) r", r=HALF_ROWS * W)
+        strips = const.tile([P, 2 * STRIP], F32)
+        strip_rows = strips[:].rearrange("q (s r) -> q s r", r=HALF_ROWS * W)
         nc.vector.memset(strip_rows[:, :, 0 : 2 * W], 0.0)
         nc.vector.memset(strip_rows[:, :, 7 * W : 8 * W], 0.0)
-        unit = const.tile([W, 2, 4, 2 * W], F32)
+        ident_bf = const.tile([P, P], BF16)
+        nc.vector.tensor_copy(out=ident_bf[:], in_=ident[:])
+        is_column = const.tile([P, W], F32)
+        nc.vector.reduce_sum(out=is_column[:], in_=ident[:].rearrange("q (w n) -> q w n", n=SLOTS), axis=mybir.AxisListType.X)
+        is_slot = const.tile([P, SLOTS], F32)
+        nc.vector.reduce_sum(out=is_slot[:], in_=ident[:].rearrange("q (w n) -> q n w", n=SLOTS), axis=mybir.AxisListType.X)
+        unit = const.tile([P, 2, 4, 2 * W], F32)
         nc.vector.tensor_scalar_mul(
             out=unit[:].rearrange("q k s (c w) -> q (k s c) w", c=2),
-            in0=ident[0:W, 0:W].unsqueeze(1).to_broadcast([W, 2 * 4 * 2, W]),
+            in0=is_column[:].unsqueeze(1).to_broadcast([P, 2 * 4 * 2, W]),
             scalar1=0.5,
         )
         for k, over_the_edge in [(0, 3), (1, 2)]:
             nc.vector.tensor_scalar_mul(
                 out=unit[:, k, over_the_edge, :].rearrange("q (c w) -> q c w", c=2),
-                in0=ident[0:W, 0:W].unsqueeze(1).to_broadcast([W, 2, W]),
+                in0=is_column[:].unsqueeze(1).to_broadcast([P, 2, W]),
                 scalar1=-0.5,
             )
-        w_f32 = const.tile([P, TERMS * B], F32)
-        nc.vector.tensor_copy(out=w_f32[:], in_=w_bf[:])
 
-        mb_rows_f32 = const.tile([P, P], F32)
-        nc.vector.tensor_copy(out=mb_rows_f32[:], in_=mb_rows[:])
-        mb_t = psum.tile([P, BANK], F32, tag="bank")
-        nc.tensor.transpose(mb_t[:, 0:P], mb_rows_f32[:], ident[:])
-        filled = set()
-        for i, (dy, dx) in enumerate(OFFSETS):
-            for n, b in enumerate(matrix_images):
-                row = (dy % HALF_ROWS) * W
-                place = strips[:, n, :].rearrange("q (s r) -> q s r", s=4)[:, :, row : row + W]
-                values = unit[:, 1 if dy > 0 else 0, :, (-dx) % W : (-dx) % W + W]
-                w_16 = w_f32[0:W, i * B + b : i * B + b + 1]
-                if (row, n) in filled:
-                    nc.vector.scalar_tensor_tensor(out=place, in0=values, scalar=w_16, in1=place, op0=ALU.mult, op1=ALU.add)
-                else:
-                    nc.vector.tensor_scalar_mul(out=place, in0=values, scalar1=w_16)
-                filled.add((row, n))
+        small = psum.tile([P, BANK], F32, tag="bank")
+        nc.tensor.matmul(
+            out=small[:, 0 : TERMS * B],
+            lhsT=ident_bf[:, W_ROW : W_ROW + 1].to_broadcast([P, P]),
+            rhs=small_rows[:, 0 : TERMS * B],
+            start=True,
+            stop=True,
+        )
+        nc.tensor.matmul(out=small[:, P : P + D_TILES], lhsT=small_rows[:], rhs=ident_bf[:, 0:D_TILES], start=True, stop=True)
+        w_f32 = const.tile([P, TERMS * B], F32)
+        nc.vector.tensor_copy(out=w_f32[:], in_=small[:, 0 : TERMS * B])
+        n_slots = len(matrix_images)
+        slot_terms = const.tile([P, TERMS, n_slots], F32)
+        nc.vector.tensor_tensor(
+            out=slot_terms[:],
+            in0=w_f32[:].rearrange("q (i b) -> q i b", b=B)[:, :, matrix_images[0] : matrix_images[0] + n_slots],
+            in1=is_slot[:, 0:n_slots].unsqueeze(1).to_broadcast([P, TERMS, n_slots]),
+            op=ALU.mult,
+        )
+        mb_sb = const.tile([P, D_TILES], F32)
+        nc.vector.tensor_copy(out=mb_sb[:], in_=small[:, P : P + D_TILES])
+        slot_w = const.tile([P, TERMS], F32)
+        nc.vector.reduce_sum(out=slot_w[:], in_=slot_terms[:], axis=mybir.AxisListType.X)
+        w_sum = const.tile([P, B], F32)
+        nc.vector.reduce_sum(out=w_sum[:], in_=w_f32[:].rearrange("p (i b) -> p b i", b=B), axis=mybir.AxisListType.X)
+        far = [i for i in range(TERMS) if abs(OFFSETS[i][0]) == REACH]
+        near = [i for i in range(TERMS) if abs(OFFSETS[i][0]) < REACH]
+        for i in [i for both in zip(far, near) for i in both]:
+            dy, dx = OFFSETS[i]
+            row = (dy % HALF_ROWS) * W
+            place = strip_rows[:, :, row : row + W]
+            values = unit[:, 1 if dy > 0 else 0, :, (-dx) % W : (-dx) % W + W]
+            if i in far[1:]:
+                nc.vector.scalar_tensor_tensor(
+                    out=place, in0=values, scalar=slot_w[:, i : i + 1], in1=place, op0=ALU.mult, op1=ALU.add
+                )
+            else:
+                nc.vector.tensor_scalar_mul(out=place, in0=values, scalar1=slot_w[:, i : i + 1])
         matrices = const.tile([P, 2 * len(matrix_images), P], F32)
-        parked = out[B - 1, 0 : W * 2 * len(matrix_images)].rearrange("(w m) h c -> w m (h c)", w=W)
+        parked = out[B - 1, 0 : 2 * P]
+
+        def park_strips():
+            nc.sync.dma_start(out=parked.rearrange("(q s) h c -> q (s h c)", s=2), in_=strips[:])
 
         def spread_matrices():
-            nc.sync.dma_start(out=parked, in_=strips[:].rearrange("q n (s r) -> q (n s) r", s=2))
+            windows = parked.rearrange("(w m) h c -> w m (h c)", w=W)[:, 0 : 2 * len(matrix_images), :]
             for h in range(HALF_ROWS):
                 start = (HALF_ROWS - h) * W
-                nc.sync.dma_start(out=matrices[h * W : (h + 1) * W, :, :], in_=parked[:, :, start : start + P])
+                nc.sync.dma_start(out=matrices[h * W : (h + 1) * W, :, :], in_=windows[:, :, start : start + P])
 
         def matrix(b, sign):
             return matrices[:, 2 * matrix_images.index(b) + sign, :]
@@ -157,7 +188,7 @@ def tile_graphaugmentation_pa_kernel(tc, x, mw, mb, attn_w, out):
         mw_scales = keep.tile([P, PASSES, C], U8, align_bytes=64)
         mw_grouped = dict()
 
-        def transpose_mw(t):
+        def transpose_mw(t, copy):
             words = mw_raw[:, t, :].bitcast(F32)
             w_t = psum.tile([P, BANK], F32, tag="bank")
             for g in range(PASSES):
@@ -167,19 +198,22 @@ def tile_graphaugmentation_pa_kernel(tc, x, mw, mb, attn_w, out):
                         words[:, 2 * P * g + u : 2 * P * (g + 1) : 2],
                         ident[:],
                     )
-            mw_grp = stage.tile([P, PASSES * P * PACK], BF16, name="mw_grp", align_bytes=64, bufs=4)
-            nc.scalar.copy(
-                out=mw_grp[:].bitcast(F32).rearrange("q (g d u) -> q g d u", g=PASSES, u=2),
+            if t % PAIR == 0:
+                mw_grouped[t] = stage.tile([P, PASSES, PAIR * P * PACK], BF16, name="mw_grp", align_bytes=64, bufs=3)
+            at = (t % PAIR) * P * PACK
+            copy(
+                out=mw_grouped[t - t % PAIR][:, :, at : at + P * PACK].bitcast(F32).rearrange("q g (d u) -> q g d u", u=2),
                 in_=w_t[:].rearrange("q (g u d) -> q g d u", g=PASSES, u=2),
             )
-            mw_grouped[t] = mw_grp
 
-        def quantise_mw(t):
+        def quantise_mw(t0, n):
+            channels = slice(t0 * P, (t0 + n) * P)
+            first = (t0 % PAIR) * P * PACK
             for g in range(PASSES):
                 nc.vector.quantize_mx(
-                    out=mw_codes[:, g, t * P : (t + 1) * P].bitcast(FP8X4),
-                    scales=mw_scales[:, g, t * P : (t + 1) * P],
-                    in_=mw_grouped[t][:, g * P * PACK : (g + 1) * P * PACK],
+                    out=mw_codes[:, g, channels].bitcast(FP8X4),
+                    scales=mw_scales[:, g, channels],
+                    in_=mw_grouped[t0 - t0 % PAIR][:, g, first : first + n * P * PACK],
                 )
 
         def mw_part(g, channels):
@@ -230,36 +264,35 @@ def tile_graphaugmentation_pa_kernel(tc, x, mw, mb, attn_w, out):
                 )
             store(b, t0, n, res)
 
-        def multiply_direct(b, t0):
+        def multiply_direct(b, t0, n):
             bank = psum.tile([P, BANK], F32, tag="bank")
-            for j in range(PAIR):
+            for j in range(n):
                 channels = slice((t0 + j) * P, (t0 + j + 1) * P)
                 mx_group(
                     bank[:, j * PIX : (j + 1) * PIX],
                     [(mw_part(g, channels), x_part(b, g, slice(0, PIX))) for g in range(PASSES)],
                 )
-            return (b, t0, bank)
+            return (b, t0, n, bank)
 
-        def start_sum(b, t0, bank):
-            ring = work.tile([P, H + 2 * REACH, PAIR, 2 * W], F32, name="ring", bufs=5)
-            for j in range(PAIR):
-                t = t0 + j
-                acc = bank[:, j * PIX : (j + 1) * PIX]
-                for ring_row, image_row, n in [(REACH, 0, H), (0, H - REACH, REACH), (REACH + H, 0, REACH)]:
+        def start_sum(b, t0, n, bank):
+            ring = work.tile([P, H + 2 * REACH, PAIR, 2 * W], F32, name="ring", bufs=5)[:, :, 0:n, :]
+            for j in range(n):
+                m = bank[:, j * PIX : (j + 1) * PIX]
+                for ring_row, image_row, rows in [(REACH, 0, H), (0, H - REACH, REACH), (REACH + H, 0, REACH)]:
                     nc.scalar.activation(
-                        out=ring[:, ring_row : ring_row + n, j, :].rearrange("p r (c w) -> p r c w", c=2),
-                        in_=acc[:, image_row * W : (image_row + n) * W]
+                        out=ring[:, ring_row : ring_row + rows, j, :].rearrange("p r (c w) -> p r c w", c=2),
+                        in_=m[:, image_row * W : (image_row + rows) * W]
                         .rearrange("p (r w) -> p r w", w=W)
                         .unsqueeze(2)
-                        .to_broadcast([P, n, 2, W]),
+                        .to_broadcast([P, rows, 2, W]),
                         func=ACT.Identity,
-                        bias=mb_sb[:, t : t + 1],
+                        bias=mb_sb[:, t0 + j : t0 + j + 1],
                         scale=1.0,
                     )
-            acc = work.tile([P, H, PAIR, W], F32, name="acc", bufs=5)
-            nc.scalar.activation(out=acc[:], in_=shifted(ring, 0), func=ACT.Copy, scale=weight(0, b))
-            res = work.tile([P, PAIR, PIX], F32, name="res2", bufs=5)
-            return (b, t0, PAIR, ring, acc, res)
+            acc = work.tile([P, H, PAIR, W], F32, name="acc", bufs=5)[:, :, 0:n, :]
+            nc.scalar.activation(out=acc, in_=shifted(ring, 0), func=ACT.Copy, scale=weight(0, b))
+            res = work.tile([P, PAIR, PIX], F32, name="res2", bufs=5)[:, 0:n, :]
+            return (b, t0, n, ring, acc, res)
 
         def split(chain):
             b, t0, n, ring, acc, res = chain
@@ -267,8 +300,8 @@ def tile_graphaugmentation_pa_kernel(tc, x, mw, mb, attn_w, out):
                 (b, t0 + j, 1, ring[:, :, j : j + 1, :], acc[:, :, j : j + 1, :], res[:, j : j + 1, :]) for j in range(n)
             ]
 
-        def plan_sums(chains):
-            for i in range(1, TERMS):
+        def plan_sums(chains, first=1):
+            for i in range(first, TERMS):
                 for chain in chains:
                     sum_steps.append((chain, i))
 
@@ -279,20 +312,24 @@ def tile_graphaugmentation_pa_kernel(tc, x, mw, mb, attn_w, out):
                 sum_steps.remove(sum_steps[0])
                 tiles -= chain[2]
 
-        def multiply(b):
-            folded = work.tile([P, 2, C], F32, name="folded", bufs=2)
-            parts = []
-            for t0, n_tiles in tile_groups(0, D_TILES - DIRECT_TILES[b], GROUP):
-                channels = slice(t0 * P, (t0 + n_tiles) * P)
-                lower = [(x_part(b, g, slice(0, P)), mw_part(g, channels)) for g in range(PASSES)]
-                upper = [(x_part(b, g, slice(P, 2 * P)), mw_part(g, channels)) for g in range(PASSES)]
-                bank_sum = psum.tile([P, BANK], F32, tag="bank")
-                mx_group(bank_sum[:, 0 : n_tiles * P], lower + upper)
-                nc.scalar.copy(out=folded[:, 0, channels], in_=bank_sum[:, 0 : n_tiles * P])
-                bank_lo = psum.tile([P, BANK], F32, tag="bank")
-                mx_group(bank_lo[:, 0 : n_tiles * P], lower)
-                parts.append((folded, channels, bank_lo[:, 0 : n_tiles * P]))
-            return parts
+        folded_tiles = dict()
+
+        def multiply_group(b, t0, n_tiles):
+            if t0 == 0:
+                folded_tiles[b] = work.tile([P, 2, C], F32, name="folded", bufs=2)
+            folded = folded_tiles[b]
+            channels = slice(t0 * P, (t0 + n_tiles) * P)
+            lower = [(x_part(b, g, slice(0, P)), mw_part(g, channels)) for g in range(PASSES)]
+            upper = [(x_part(b, g, slice(P, 2 * P)), mw_part(g, channels)) for g in range(PASSES)]
+            bank_sum = psum.tile([P, BANK], F32, tag="bank")
+            mx_group(bank_sum[:, 0 : n_tiles * P], lower + upper)
+            nc.scalar.copy(out=folded[:, 0, channels], in_=bank_sum[:, 0 : n_tiles * P])
+            bank_lo = psum.tile([P, BANK], F32, tag="bank")
+            mx_group(bank_lo[:, 0 : n_tiles * P], lower)
+            return (folded, channels, bank_lo[:, 0 : n_tiles * P])
+
+        def matrix_groups(b, size):
+            return tile_groups(0, D_TILES - DIRECT_TILES[b], size)
 
         def subtract(folded, channels, lo):
             nc.vector.scalar_tensor_tensor(
@@ -338,12 +375,12 @@ def tile_graphaugmentation_pa_kernel(tc, x, mw, mb, attn_w, out):
             store(b, t0, n_tiles, res)
 
 
+        park_strips()
+        load_x(2)
+        spread_matrices()
+        for b in range(3, B):
+            load_x(b)
         regroup_x(0, nc.vector.tensor_copy)
-        mb_sb = const.tile([P, D_TILES], F32)
-        nc.vector.tensor_copy(out=mb_sb[:], in_=mb_t[:, 0:D_TILES])
-        w_sum = const.tile([P, B], F32)
-        nc.vector.reduce_sum(out=w_sum[:], in_=w_f32[:].rearrange("p (i b) -> p b i", b=B), axis=mybir.AxisListType.X)
-        quantise_x(0)
         mb_w = const.tile([P, B, D_TILES], F32)
         nc.vector.tensor_tensor(
             out=mb_w[:],
@@ -351,52 +388,53 @@ def tile_graphaugmentation_pa_kernel(tc, x, mw, mb, attn_w, out):
             in1=w_sum[:].unsqueeze(2).to_broadcast([P, B, D_TILES]),
             op=ALU.mult,
         )
-        spread_matrices()
-        for b in range(3, B):
-            load_x(b)
-        for t in range(D_TILES):
-            transpose_mw(t)
-            if t > 0:
-                quantise_mw(t - 1)
+        quantise_x(0)
+        for t in range(4):
+            transpose_mw(t, nc.scalar.copy)
+        for t in (0, 1):
+            quantise_mw(t, 1)
+        chains = [start_sum(*multiply_direct(0, t, 1)) for t in (0, 1)]
         regroup_x(1, nc.vector.tensor_copy)
-        quantise_mw(D_TILES - 1)
+        quantise_mw(2, 2)
         quantise_x(1)
-
-        products = [multiply_direct(0, t0) for t0 in range(0, D_TILES, PAIR)]
-        plan_sums([start_sum(*product) for product in products[:2]])
-
-        folded = dict()
-        folded[1] = multiply(1)
+        sum_steps.extend([(chains[0], 1), (chains[0], 2), (chains[1], 1), (chains[1], 2)])
+        plan_sums(chains, 3)
+        for t in (4, 5):
+            transpose_mw(t, nc.scalar.copy)
+        product = multiply_direct(0, 2, 2)
+        add_terms(2)
+        for t in (6, 7):
+            transpose_mw(t, nc.scalar.copy)
+        m1 = [multiply_group(1, 0, 4)]
+        chain1 = start_sum(*product)
         regroup_x(2, nc.vector.tensor_copy)
-        plan_sums([start_sum(*product) for product in products[2:]])
+        quantise_mw(4, 2)
         add_terms(2)
+        quantise_mw(6, 2)
+        m1.append(multiply_group(1, 4, 4))
         quantise_x(2)
-
-        for part in folded[1]:
-            add_terms(4)
-            subtract(*part)
-        folded[2] = multiply(2)
-        add_terms(4)
-        regroup_x(3, nc.vector.tensor_copy)
         add_terms(2)
-        quantise_x(3)
-        for part in folded[2]:
-            add_terms(2)
-            subtract(*part)
-        add_terms(4)
+        subtract(*m1[0])
+        add_terms(2)
+        subtract(*m1[1])
+        plan_sums([chain1])
+
         for b in range(1, B):
-            if b + 3 < B:
-                regroup_x(b + 3, nc.scalar.copy)
-            if b > 1 and b + 1 < B:
-                folded[b + 1] = multiply(b + 1)
-            if b == 2:
-                plan_sums(split(start_sum(*multiply_direct(3, 6))))
-            for g, (t0, n_tiles) in enumerate(tile_groups(0, D_TILES - DIRECT_TILES[b], GROUP if b + 1 < B else PAIR)):
-                if b > 1 and b + 1 < B:
-                    subtract(*folded[b + 1][g])
-                part = apply_matrices(b, folded[b][0][0], t0, n_tiles)
-                add_terms(8 if b == 4 and g == 0 else 4)
+            nxt = matrix_groups(b + 1, GROUP) if b + 1 < B else []
+            for g, (t0, n_tiles) in enumerate(matrix_groups(b, GROUP if b + 1 < B else PAIR)):
+                part = apply_matrices(b, folded_tiles[b], t0, n_tiles)
+                new = multiply_group(b + 1, *nxt[g]) if nxt else None
+                if g == 0 and b + 2 < B:
+                    regroup_x(b + 2, nc.scalar.copy)
+                if g == 1 and b < 3:
+                    plan_sums([start_sum(*multiply_direct(0, 2 + 2 * b, 2))])
+                if g == 1 and b == 3:
+                    plan_sums(split(start_sum(*multiply_direct(3, 6, 2))))
+                add_terms(4 if new else 2)
+                if g == 1 and b + 2 < B:
+                    quantise_x(b + 2)
                 unfold(*part)
-                if g == 0 and b + 3 < B:
-                    quantise_x(b + 3)
+                if new:
+                    add_terms(2 + 2 * g)
+                    subtract(*new)
         add_terms(70)

@@ -62,18 +62,24 @@ def tile_graphaugmentation_pa_kernel(tc, x, mw, mb, attn_w, out):
                 in_=x[b].rearrange("(g q t) h w -> q g (t h w)", q=P, t=PACK),
             )
 
+        def load_x_pass(b, g):
+            nc.sync.dma_start(
+                out=x_raw[b][:, g * PACK * PIX : (g + 1) * PACK * PIX],
+                in_=x[b, g * K_PASS : (g + 1) * K_PASS].rearrange("(q t) h w -> q (t h w)", t=PACK),
+            )
+
         small_rows = const.tile([P, P], BF16)
         nc.vector.memset(small_rows[:], 0.0)
-        nc.scalar.dma_start(out=small_rows[W_ROW : W_ROW + 1, 0 : TERMS * B], in_=attn_w.rearrange("(o i) b -> o (i b)", o=1))
-        nc.scalar.dma_start(out=small_rows[0:D_TILES, :], in_=mb.rearrange("(t p) -> t p", p=P))
-
         def load_mw(t0, n):
             nc.sync.dma_start(
                 out=mw_raw[:, t0 : t0 + n, :],
                 in_=mw[t0 * P : (t0 + n) * P, :].rearrange("(t p) c -> p t c", p=P),
             )
 
-        load_x(0)
+        load_x_pass(0, 0)
+        nc.sync.dma_start(out=small_rows[W_ROW : W_ROW + 1, 0 : TERMS * B], in_=attn_w.rearrange("(o i) b -> o (i b)", o=1))
+        nc.sync.dma_start(out=small_rows[0:D_TILES, :], in_=mb.rearrange("(t p) -> t p", p=P))
+        load_x_pass(0, 1)
         load_mw(0, 1)
         load_mw(1, 1)
         load_mw(2, 2)
@@ -323,15 +329,17 @@ def tile_graphaugmentation_pa_kernel(tc, x, mw, mb, attn_w, out):
             upper = [(x_part(b, g, slice(P, 2 * P)), mw_part(g, channels)) for g in range(PASSES)]
             bank_sum = psum.tile([P, BANK], F32, tag="bank")
             mx_group(bank_sum[:, 0 : n_tiles * P], lower + upper)
-            nc.scalar.copy(out=folded[:, 0, channels], in_=bank_sum[:, 0 : n_tiles * P])
             bank_lo = psum.tile([P, BANK], F32, tag="bank")
             mx_group(bank_lo[:, 0 : n_tiles * P], lower)
-            return (folded, channels, bank_lo[:, 0 : n_tiles * P])
+            return (folded, channels, bank_sum[:, 0 : n_tiles * P], bank_lo[:, 0 : n_tiles * P])
+
+        def keep_sum(folded, channels, total, lo):
+            nc.scalar.copy(out=folded[:, 0, channels], in_=total)
 
         def matrix_groups(b, size):
             return tile_groups(0, D_TILES - DIRECT_TILES[b], size)
 
-        def subtract(folded, channels, lo):
+        def subtract(folded, channels, total, lo):
             nc.vector.scalar_tensor_tensor(
                 out=folded[:, 1, channels], in0=lo, scalar=2.0, in1=folded[:, 0, channels], op0=ALU.mult, op1=ALU.subtract
             )
@@ -361,7 +369,7 @@ def tile_graphaugmentation_pa_kernel(tc, x, mw, mb, attn_w, out):
                 )
             return (b, t0, n_tiles, u_sb, bank_v)
 
-        def unfold(b, t0, n_tiles, u_sb, bank_v):
+        def unfold(b, t0, n_tiles, u_sb, bank_v, behind_half):
             res = work.tile([P, n_tiles, PIX], F32, name="res_folded%d" % n_tiles, bufs=4 if n_tiles == PAIR else 3)
             for half, sign in enumerate((1.0, -1.0)):
                 nc.vector.scalar_tensor_tensor(
@@ -372,6 +380,7 @@ def tile_graphaugmentation_pa_kernel(tc, x, mw, mb, attn_w, out):
                     op0=ALU.mult,
                     op1=ALU.add,
                 )
+                behind_half()
             store(b, t0, n_tiles, res)
 
 
@@ -397,8 +406,7 @@ def tile_graphaugmentation_pa_kernel(tc, x, mw, mb, attn_w, out):
         regroup_x(1, nc.vector.tensor_copy)
         quantise_mw(2, 2)
         quantise_x(1)
-        sum_steps.extend([(chains[0], 1), (chains[0], 2), (chains[1], 1), (chains[1], 2)])
-        plan_sums(chains, 3)
+        plan_sums(chains)
         for t in (4, 5):
             transpose_mw(t, nc.scalar.copy)
         product = multiply_direct(0, 2, 2)
@@ -406,35 +414,43 @@ def tile_graphaugmentation_pa_kernel(tc, x, mw, mb, attn_w, out):
         for t in (6, 7):
             transpose_mw(t, nc.scalar.copy)
         m1 = [multiply_group(1, 0, 4)]
+        keep_sum(*m1[0])
         chain1 = start_sum(*product)
         regroup_x(2, nc.vector.tensor_copy)
         quantise_mw(4, 2)
         add_terms(2)
         quantise_mw(6, 2)
         m1.append(multiply_group(1, 4, 4))
+        keep_sum(*m1[1])
         quantise_x(2)
         add_terms(2)
         subtract(*m1[0])
         add_terms(2)
         subtract(*m1[1])
         plan_sums([chain1])
+        add_terms(2)
 
         for b in range(1, B):
             nxt = matrix_groups(b + 1, GROUP) if b + 1 < B else []
             for g, (t0, n_tiles) in enumerate(matrix_groups(b, GROUP if b + 1 < B else PAIR)):
                 part = apply_matrices(b, folded_tiles[b], t0, n_tiles)
+                direct = None
+                if g == 1 and b <= 3:
+                    direct = multiply_direct(*((0, 2 + 2 * b, 2) if b < 3 else (3, 6, 2)))
                 new = multiply_group(b + 1, *nxt[g]) if nxt else None
                 if g == 0 and b + 2 < B:
                     regroup_x(b + 2, nc.scalar.copy)
-                if g == 1 and b < 3:
-                    plan_sums([start_sum(*multiply_direct(0, 2 + 2 * b, 2))])
-                if g == 1 and b == 3:
-                    plan_sums(split(start_sum(*multiply_direct(3, 6, 2))))
-                add_terms(4 if new else 2)
-                if g == 1 and b + 2 < B:
-                    quantise_x(b + 2)
-                unfold(*part)
+                if direct:
+                    chain = start_sum(*direct)
+                    plan_sums(split(chain) if b == 3 else [chain])
                 if new:
-                    add_terms(2 + 2 * g)
+                    keep_sum(*new)
+                unfold(*part, lambda: add_terms(2 if new else 1))
+                if new and g == 1:
+                    if b + 2 < B:
+                        quantise_x(b + 2)
+                    add_terms(2)
+                if new:
                     subtract(*new)
+                    add_terms(2)
         add_terms(70)

@@ -29,6 +29,8 @@ SLOTS = P // W
 GROUP = 4
 PAIR = 2
 
+LAST_GROUPS = ((0, 2), (2, 2), (4, 2), (6, 1), (7, 1))
+
 FLOPS = 2 * B * C * C * PIX + 2 * TERMS * B * C * PIX
 
 DIRECT_TILES = (8, 0, 0, 2, 0, 0)
@@ -84,8 +86,6 @@ def tile_graphaugmentation_pa_kernel(tc, x, mw, mb, attn_w, out):
         load_mw(1, 1)
         load_mw(2, 2)
         load_x(1)
-        load_mw(4, 2)
-        load_mw(6, 2)
 
         ident = const.tile([P, P], F32)
         make_identity(nc, ident[:])
@@ -161,11 +161,13 @@ def tile_graphaugmentation_pa_kernel(tc, x, mw, mb, attn_w, out):
         def park_strips():
             nc.sync.dma_start(out=parked.rearrange("(q s) h c -> q (s h c)", s=2), in_=strips[:])
 
-        def spread_matrices():
-            windows = parked.rearrange("(w m) h c -> w m (h c)", w=W)[:, 0 : 2 * len(matrix_images), :]
+        def spread_matrices(images):
+            first = 2 * matrix_images.index(images[0])
+            m = slice(first, first + 2 * len(images))
+            windows = parked.rearrange("(w m) h c -> w m (h c)", w=W)
             for h in range(HALF_ROWS):
                 start = (HALF_ROWS - h) * W
-                nc.sync.dma_start(out=matrices[h * W : (h + 1) * W, :, :], in_=windows[:, :, start : start + P])
+                nc.sync.dma_start(out=matrices[h * W : (h + 1) * W, m, :], in_=windows[:, m, start : start + P])
 
         def matrix(b, sign):
             return matrices[:, 2 * matrix_images.index(b) + sign, :]
@@ -357,7 +359,7 @@ def tile_graphaugmentation_pa_kernel(tc, x, mw, mb, attn_w, out):
                         start=True,
                         stop=True,
                     )
-            u_sb = work.tile([P, GROUP, P], F32, name="u_sb", bufs=3)
+            u_sb = work.tile([P, GROUP, P], F32, name="u_sb", bufs=4)
             for j in range(n_tiles):
                 t = t0 + j
                 nc.scalar.activation(
@@ -370,7 +372,7 @@ def tile_graphaugmentation_pa_kernel(tc, x, mw, mb, attn_w, out):
             return (b, t0, n_tiles, u_sb, bank_v)
 
         def unfold(b, t0, n_tiles, u_sb, bank_v, behind_half):
-            res = work.tile([P, n_tiles, PIX], F32, name="res_folded%d" % n_tiles, bufs=4 if n_tiles == PAIR else 3)
+            res = work.tile([P, n_tiles, PIX], F32, name="res_folded%d" % n_tiles, bufs=4 if n_tiles < GROUP else 3)
             for half, sign in enumerate((1.0, -1.0)):
                 nc.vector.scalar_tensor_tensor(
                     out=res[:, :, half * P : (half + 1) * P],
@@ -385,9 +387,13 @@ def tile_graphaugmentation_pa_kernel(tc, x, mw, mb, attn_w, out):
 
 
         park_strips()
+        load_mw(4, 2)
+        load_mw(6, 2)
         load_x(2)
-        spread_matrices()
-        for b in range(3, B):
+        spread_matrices(matrix_images[:2])
+        load_x(3)
+        spread_matrices(matrix_images[2:])
+        for b in range(4, B):
             load_x(b)
         regroup_x(0, nc.vector.tensor_copy)
         mb_w = const.tile([P, B, D_TILES], F32)
@@ -432,7 +438,7 @@ def tile_graphaugmentation_pa_kernel(tc, x, mw, mb, attn_w, out):
 
         for b in range(1, B):
             nxt = matrix_groups(b + 1, GROUP) if b + 1 < B else []
-            for g, (t0, n_tiles) in enumerate(matrix_groups(b, GROUP if b + 1 < B else PAIR)):
+            for g, (t0, n_tiles) in enumerate((matrix_groups(b, GROUP) if b + 1 < B else LAST_GROUPS)):
                 part = apply_matrices(b, folded_tiles[b], t0, n_tiles)
                 direct = None
                 if g == 1 and b <= 3:
@@ -445,12 +451,11 @@ def tile_graphaugmentation_pa_kernel(tc, x, mw, mb, attn_w, out):
                     plan_sums(split(chain) if b == 3 else [chain])
                 if new:
                     keep_sum(*new)
-                unfold(*part, lambda: add_terms(2 if new else 1))
-                if new and g == 1:
-                    if b + 2 < B:
-                        quantise_x(b + 2)
-                    add_terms(2)
+                unfold(*part, lambda: add_terms(2 if new else 2))
                 if new:
                     subtract(*new)
+                    add_terms(2)
+                if g == 0 and b + 2 < B:
+                    quantise_x(b + 2)
                     add_terms(2)
         add_terms(70)

@@ -117,6 +117,28 @@ def tile_graphaugmentation_pa_kernel(tc, x, mw, mb, attn_w, out):
                 scalar1=-0.5,
             )
 
+        x_codes = [keep.tile([P, PASSES, PIX], U32, name="x_codes%d" % b, align_bytes=64) for b in range(B)]
+        x_scales = [keep.tile([P, PASSES, PIX], U8, name="x_scales%d" % b, align_bytes=64) for b in range(B)]
+        grouped = dict()
+
+        def regroup_x(b, copy, passes=range(PASSES)):
+            if b not in grouped:
+                grouped[b] = stage.tile([P, PASSES, PIX * PACK], BF16, name="x_grp", align_bytes=64)
+            for g in passes:
+                copy(
+                    out=grouped[b][:, g, :].rearrange("q (c i t) -> q c t i", i=4, t=PACK),
+                    in_=x_raw[b][:].rearrange("q (g t c i) -> q g c t i", g=PASSES, t=PACK, i=4)[:, g],
+                )
+
+        def quantise_x(b):
+            nc.vector.quantize_mx(
+                out=x_codes[b][:].rearrange("q g c -> q (g c)").bitcast(FP8X4),
+                scales=x_scales[b][:].rearrange("q g c -> q (g c)"),
+                in_=grouped[b][:].rearrange("q g c -> q (g c)"),
+            )
+
+        regroup_x(0, nc.vector.tensor_copy, [0])
+
         small = psum.tile([P, BANK], F32, tag="bank")
         nc.tensor.matmul(
             out=small[:, 0 : TERMS * B],
@@ -171,26 +193,6 @@ def tile_graphaugmentation_pa_kernel(tc, x, mw, mb, attn_w, out):
 
         def matrix(b, sign):
             return matrices[:, 2 * matrix_images.index(b) + sign, :]
-
-        x_codes = [keep.tile([P, PASSES, PIX], U32, name="x_codes%d" % b, align_bytes=64) for b in range(B)]
-        x_scales = [keep.tile([P, PASSES, PIX], U8, name="x_scales%d" % b, align_bytes=64) for b in range(B)]
-        grouped = dict()
-
-        def regroup_x(b, copy):
-            x_grp = stage.tile([P, PASSES, PIX * PACK], BF16, name="x_grp", align_bytes=64)
-            for g in range(PASSES):
-                copy(
-                    out=x_grp[:, g, :].rearrange("q (c i t) -> q c t i", i=4, t=PACK),
-                    in_=x_raw[b][:].rearrange("q (g t c i) -> q g c t i", g=PASSES, t=PACK, i=4)[:, g],
-                )
-            grouped[b] = x_grp
-
-        def quantise_x(b):
-            nc.vector.quantize_mx(
-                out=x_codes[b][:].rearrange("q g c -> q (g c)").bitcast(FP8X4),
-                scales=x_scales[b][:].rearrange("q g c -> q (g c)"),
-                in_=grouped[b][:].rearrange("q g c -> q (g c)"),
-            )
 
         mw_codes = keep.tile([P, PASSES, C], U32, align_bytes=64)
         mw_scales = keep.tile([P, PASSES, C], U8, align_bytes=64)
@@ -282,7 +284,7 @@ def tile_graphaugmentation_pa_kernel(tc, x, mw, mb, attn_w, out):
                 )
             return (b, t0, n, bank)
 
-        def start_sum(b, t0, n, bank):
+        def fill_ring(b, t0, n, bank):
             ring = work.tile([P, H + 2 * REACH, PAIR, 2 * W], F32, name="ring", bufs=5)[:, :, 0:n, :]
             for j in range(n):
                 m = bank[:, j * PIX : (j + 1) * PIX]
@@ -297,6 +299,9 @@ def tile_graphaugmentation_pa_kernel(tc, x, mw, mb, attn_w, out):
                         bias=mb_sb[:, t0 + j : t0 + j + 1],
                         scale=1.0,
                     )
+            return (b, t0, n, ring)
+
+        def first_term(b, t0, n, ring):
             acc = work.tile([P, H, PAIR, W], F32, name="acc", bufs=5)[:, :, 0:n, :]
             nc.scalar.activation(out=acc, in_=shifted(ring, 0), func=ACT.Copy, scale=weight(0, b))
             res = work.tile([P, PAIR, PIX], F32, name="res2", bufs=5)[:, 0:n, :]
@@ -386,8 +391,8 @@ def tile_graphaugmentation_pa_kernel(tc, x, mw, mb, attn_w, out):
             store(b, t0, n_tiles, res)
 
 
-        park_strips()
         load_mw(4, 2)
+        park_strips()
         load_mw(6, 2)
         load_x(2)
         spread_matrices(matrix_images[:2])
@@ -395,7 +400,7 @@ def tile_graphaugmentation_pa_kernel(tc, x, mw, mb, attn_w, out):
         spread_matrices(matrix_images[2:])
         for b in range(4, B):
             load_x(b)
-        regroup_x(0, nc.vector.tensor_copy)
+        regroup_x(0, nc.vector.tensor_copy, [1])
         mb_w = const.tile([P, B, D_TILES], F32)
         nc.vector.tensor_tensor(
             out=mb_w[:],
@@ -408,32 +413,33 @@ def tile_graphaugmentation_pa_kernel(tc, x, mw, mb, attn_w, out):
             transpose_mw(t, nc.scalar.copy)
         for t in (0, 1):
             quantise_mw(t, 1)
-        chains = [start_sum(*multiply_direct(0, t, 1)) for t in (0, 1)]
+        ring = fill_ring(*multiply_direct(0, 0, 2))
         regroup_x(1, nc.vector.tensor_copy)
         quantise_mw(2, 2)
         quantise_x(1)
-        plan_sums(chains)
-        for t in (4, 5):
-            transpose_mw(t, nc.scalar.copy)
+        transpose_mw(4, nc.scalar.copy)
+        transpose_mw(5, nc.vector.tensor_copy)
+        plan_sums([first_term(*ring)])
         product = multiply_direct(0, 2, 2)
-        add_terms(2)
+        quantise_mw(4, 2)
         for t in (6, 7):
             transpose_mw(t, nc.scalar.copy)
         m1 = [multiply_group(1, 0, 4)]
+        regroup_x(2, nc.scalar.copy, [1])
         keep_sum(*m1[0])
-        chain1 = start_sum(*product)
-        regroup_x(2, nc.vector.tensor_copy)
-        quantise_mw(4, 2)
-        add_terms(2)
+        ring = fill_ring(*product)
+        regroup_x(2, nc.vector.tensor_copy, [0])
         quantise_mw(6, 2)
+        add_terms(2)
         m1.append(multiply_group(1, 4, 4))
         keep_sum(*m1[1])
-        quantise_x(2)
+        plan_sums([first_term(*ring)])
         add_terms(2)
         subtract(*m1[0])
         add_terms(2)
+        quantise_x(2)
+        add_terms(2)
         subtract(*m1[1])
-        plan_sums([chain1])
         add_terms(2)
 
         for b in range(1, B):
@@ -444,13 +450,17 @@ def tile_graphaugmentation_pa_kernel(tc, x, mw, mb, attn_w, out):
                 if g == 1 and b <= 3:
                     direct = multiply_direct(*((0, 2 + 2 * b, 2) if b < 3 else (3, 6, 2)))
                 new = multiply_group(b + 1, *nxt[g]) if nxt else None
-                if g == 0 and b + 2 < B:
-                    regroup_x(b + 2, nc.scalar.copy)
+                ahead = g == 0 and b + 2 < B
+                if ahead:
+                    regroup_x(b + 2, nc.scalar.copy, [0])
                 if direct:
-                    chain = start_sum(*direct)
-                    plan_sums(split(chain) if b == 3 else [chain])
+                    ring = fill_ring(*direct)
                 if new:
                     keep_sum(*new)
+                if ahead:
+                    regroup_x(b + 2, nc.scalar.copy, [1])
+                if direct:
+                    plan_sums([first_term(*ring)])
                 unfold(*part, lambda: add_terms(2 if new else 2))
                 if new:
                     subtract(*new)

from contextlib import ExitStack

from concourse import mybir
from concourse.masks import make_identity

F32 = mybir.dt.float32
BF16 = mybir.dt.bfloat16
U32 = mybir.dt.uint32
U8 = mybir.dt.uint8
FP8X4 = mybir.dt.float8_e4m3fn_x4
ACT = mybir.ActivationFunctionType
ALU = mybir.AluOpType

P = 128
PACK = 4
K_PASS = P * PACK
BANK = 512

B, C, H, W = 6, 1024, 16, 16
PIX = H * W
HALF_ROWS = H // 2
PASSES = C // K_PASS
D_TILES = C // P
OFFSETS = [(-4, -4), (-4, -1), (-4, 2), (-3, 4), (-2, -3), (2, 3), (3, -2), (4, 4)]
TERMS = len(OFFSETS)
REACH = 4
W_ROW = D_TILES
SLOTS = P // W
GROUP = 4
PAIR = 2

LAST_GROUPS = ((0, 2), (2, 2), (4, 2), (6, 1), (7, 1))

FLOPS = 2 * B * C * C * PIX + 2 * TERMS * B * C * PIX

DIRECT_TILES = (8, 0, 0, 2, 0, 0)


def by_matrix(b):
    return DIRECT_TILES[b] < D_TILES


def tile_groups(first, last, size):
    return [(t, min(size, last - t)) for t in range(first, last, size)]


def tile_graphaugmentation_pa_kernel(tc, x, mw, mb, attn_w, out):
    nc = tc.nc
    matrix_images = [b for b in range(B) if by_matrix(b)]
    with ExitStack() as stack:
        const = stack.enter_context(tc.tile_pool(name="const", bufs=1))
        keep = stack.enter_context(tc.tile_pool(name="keep", bufs=1))
        stage = stack.enter_context(tc.tile_pool(name="stage", bufs=2))
        work = stack.enter_context(tc.tile_pool(name="work", bufs=2))
        psum = stack.enter_context(tc.psum_pool(name="psum", bufs=8))
        stack.enter_context(tc.manual_schedule())

        x_raw = [keep.tile([P, PASSES * PACK * PIX], BF16, name="x_raw%d" % b) for b in range(B)]
        mw_raw = keep.tile([P, D_TILES, C], BF16)

        def load_x(b):
            nc.sync.dma_start(
                out=x_raw[b][:].rearrange("q (g r) -> q g r", g=PASSES),
                in_=x[b].rearrange("(g q t) h w -> q g (t h w)", q=P, t=PACK),
            )

        def load_x_pass(b, g):
            nc.sync.dma_start(
                out=x_raw[b][:, g * PACK * PIX : (g + 1) * PACK * PIX],
                in_=x[b, g * K_PASS : (g + 1) * K_PASS].rearrange("(q t) h w -> q (t h w)", t=PACK),
            )

        small_rows = const.tile([P, P], BF16)
        nc.vector.memset(small_rows[:], 0.0)
        def load_mw(t0, n):
            nc.sync.dma_start(
                out=mw_raw[:, t0 : t0 + n, :],
                in_=mw[t0 * P : (t0 + n) * P, :].rearrange("(t p) c -> p t c", p=P),
            )

        load_x_pass(0, 0)
        nc.sync.dma_start(out=small_rows[W_ROW : W_ROW + 1, 0 : TERMS * B], in_=attn_w.rearrange("(o i) b -> o (i b)", o=1))
        nc.sync.dma_start(out=small_rows[0:D_TILES, :], in_=mb.rearrange("(t p) -> t p", p=P))
        load_x_pass(0, 1)
        load_mw(0, 1)
        load_mw(1, 1)
        load_mw(2, 2)
        load_x(1)

        ident = const.tile([P, P], F32)
        make_identity(nc, ident[:])

        def weight(i, b):
            return w_f32[:, i * B + b : i * B + b + 1]

        STRIP = 2 * HALF_ROWS * W
        strips = const.tile([P, 2 * STRIP], F32)
        strip_rows = strips[:].rearrange("q (s r) -> q s r", r=HALF_ROWS * W)
        nc.vector.memset(strip_rows[:, :, 0 : 2 * W], 0.0)
        nc.vector.memset(strip_rows[:, :, 7 * W : 8 * W], 0.0)
        ident_bf = const.tile([P, P], BF16)
        nc.vector.tensor_copy(out=ident_bf[:], in_=ident[:])
        is_column = const.tile([P, W], F32)
        nc.vector.reduce_sum(out=is_column[:], in_=ident[:].rearrange("q (w n) -> q w n", n=SLOTS), axis=mybir.AxisListType.X)
        is_slot = const.tile([P, SLOTS], F32)
        nc.vector.reduce_sum(out=is_slot[:], in_=ident[:].rearrange("q (w n) -> q n w", n=SLOTS), axis=mybir.AxisListType.X)
        unit = const.tile([P, 2, 4, 2 * W], F32)
        nc.vector.tensor_scalar_mul(
            out=unit[:].rearrange("q k s (c w) -> q (k s c) w", c=2),
            in0=is_column[:].unsqueeze(1).to_broadcast([P, 2 * 4 * 2, W]),
            scalar1=0.5,
        )
        for k, over_the_edge in [(0, 3), (1, 2)]:
            nc.vector.tensor_scalar_mul(
                out=unit[:, k, over_the_edge, :].rearrange("q (c w) -> q c w", c=2),
                in0=is_column[:].unsqueeze(1).to_broadcast([P, 2, W]),
                scalar1=-0.5,
            )

        x_codes = [keep.tile([P, PASSES, PIX], U32, name="x_codes%d" % b, align_bytes=64) for b in range(B)]
        x_scales = [keep.tile([P, PASSES, PIX], U8, name="x_scales%d" % b, align_bytes=64) for b in range(B)]
        grouped = dict()

        def regroup_x(b, copy, passes=range(PASSES)):
            if b not in grouped:
                grouped[b] = stage.tile([P, PASSES, PIX * PACK], BF16, name="x_grp", align_bytes=64)
            for g in passes:
                copy(
                    out=grouped[b][:, g, :].rearrange("q (c i t) -> q c t i", i=4, t=PACK),
                    in_=x_raw[b][:].rearrange("q (g t c i) -> q g c t i", g=PASSES, t=PACK, i=4)[:, g],
                )

        def quantise_x(b):
            nc.vector.quantize_mx(
                out=x_codes[b][:].rearrange("q g c -> q (g c)").bitcast(FP8X4),
                scales=x_scales[b][:].rearrange("q g c -> q (g c)"),
                in_=grouped[b][:].rearrange("q g c -> q (g c)"),
            )

        regroup_x(0, nc.vector.tensor_copy, [0])

        small = psum.tile([P, BANK], F32, tag="bank")
        nc.tensor.matmul(
            out=small[:, 0 : TERMS * B],
            lhsT=ident_bf[:, W_ROW : W_ROW + 1].to_broadcast([P, P]),
            rhs=small_rows[:, 0 : TERMS * B],
            start=True,
            stop=True,
        )
        nc.tensor.matmul(out=small[:, P : P + D_TILES], lhsT=small_rows[:], rhs=ident_bf[:, 0:D_TILES], start=True, stop=True)
        w_f32 = const.tile([P, TERMS * B], F32)
        nc.vector.tensor_copy(out=w_f32[:], in_=small[:, 0 : TERMS * B])
        n_slots = len(matrix_images)
        slot_terms = const.tile([P, TERMS, n_slots], F32)
        nc.vector.tensor_tensor(
            out=slot_terms[:],
            in0=w_f32[:].rearrange("q (i b) -> q i b", b=B)[:, :, matrix_images[0] : matrix_images[0] + n_slots],
            in1=is_slot[:, 0:n_slots].unsqueeze(1).to_broadcast([P, TERMS, n_slots]),
            op=ALU.mult,
        )
        mb_sb = const.tile([P, D_TILES], F32)
        nc.vector.tensor_copy(out=mb_sb[:], in_=small[:, P : P + D_TILES])
        slot_w = const.tile([P, TERMS], F32)
        nc.vector.reduce_sum(out=slot_w[:], in_=slot_terms[:], axis=mybir.AxisListType.X)
        w_sum = const.tile([P, B], F32)
        nc.vector.reduce_sum(out=w_sum[:], in_=w_f32[:].rearrange("p (i b) -> p b i", b=B), axis=mybir.AxisListType.X)
        far = [i for i in range(TERMS) if abs(OFFSETS[i][0]) == REACH]
        near = [i for i in range(TERMS) if abs(OFFSETS[i][0]) < REACH]
        for i in [i for both in zip(far, near) for i in both]:
            dy, dx = OFFSETS[i]
            row = (dy % HALF_ROWS) * W
            place = strip_rows[:, :, row : row + W]
            values = unit[:, 1 if dy > 0 else 0, :, (-dx) % W : (-dx) % W + W]
            if i in far[1:]:
                nc.vector.scalar_tensor_tensor(
                    out=place, in0=values, scalar=slot_w[:, i : i + 1], in1=place, op0=ALU.mult, op1=ALU.add
                )
            else:
                nc.vector.tensor_scalar_mul(out=place, in0=values, scalar1=slot_w[:, i : i + 1])
        matrices = const.tile([P, 2 * len(matrix_images), P], F32)
        parked = out[B - 1, 0 : 2 * P]

        def park_strips():
            nc.sync.dma_start(out=parked.rearrange("(q s) h c -> q (s h c)", s=2), in_=strips[:])

        def spread_matrices(images):
            first = 2 * matrix_images.index(images[0])
            m = slice(first, first + 2 * len(images))
            windows = parked.rearrange("(w m) h c -> w m (h c)", w=W)
            for h in range(HALF_ROWS):
                start = (HALF_ROWS - h) * W
                nc.sync.dma_start(out=matrices[h * W : (h + 1) * W, m, :], in_=windows[:, m, start : start + P])

        def matrix(b, sign):
            return matrices[:, 2 * matrix_images.index(b) + sign, :]

        mw_codes = keep.tile([P, PASSES, C], U32, align_bytes=64)
        mw_scales = keep.tile([P, PASSES, C], U8, align_bytes=64)
        mw_grouped = dict()

        def transpose_mw(t, copy):
            words = mw_raw[:, t, :].bitcast(F32)
            w_t = psum.tile([P, BANK], F32, tag="bank")
            for g in range(PASSES):
                for u in range(2):
                    nc.tensor.transpose(
                        w_t[:, (2 * g + u) * P : (2 * g + u + 1) * P],
                        words[:, 2 * P * g + u : 2 * P * (g + 1) : 2],
                        ident[:],
                    )
            if t % PAIR == 0:
                mw_grouped[t] = stage.tile([P, PASSES, PAIR * P * PACK], BF16, name="mw_grp", align_bytes=64, bufs=3)
            at = (t % PAIR) * P * PACK
            copy(
                out=mw_grouped[t - t % PAIR][:, :, at : at + P * PACK].bitcast(F32).rearrange("q g (d u) -> q g d u", u=2),
                in_=w_t[:].rearrange("q (g u d) -> q g d u", g=PASSES, u=2),
            )

        def quantise_mw(t0, n):
            channels = slice(t0 * P, (t0 + n) * P)
            first = (t0 % PAIR) * P * PACK
            for g in range(PASSES):
                nc.vector.quantize_mx(
                    out=mw_codes[:, g, channels].bitcast(FP8X4),
                    scales=mw_scales[:, g, channels],
                    in_=mw_grouped[t0 - t0 % PAIR][:, g, first : first + n * P * PACK],
                )

        def mw_part(g, channels):
            return (mw_codes[:, g, channels], mw_scales[:, g, channels])

        def x_part(b, g, pixels):
            return (x_codes[b][:, g, pixels], x_scales[b][:, g, pixels])

        def mx_group(acc, pairs):
            for k, (still, moving) in enumerate(pairs):
                nc.tensor.matmul_mx(
                    out=acc,
                    lhsT=still[0].bitcast(FP8X4),
                    lhsT_scale=still[1],
                    rhs=moving[0].bitcast(FP8X4),
                    rhs_scale=moving[1],
                    start=(k == 0),
                    stop=(k == len(pairs) - 1),
                )

        def store(b, t0, n, res):
            nc.sync.dma_start(
                out=out[b, t0 * P : (t0 + n) * P].rearrange("(j p) h w -> p j (h w)", p=P),
                in_=res[:, :, :],
            )

        def shifted(ring, i):
            dy, dx = OFFSETS[i]
            return ring[:, REACH - dy : REACH - dy + H, :, (-dx) % W : (-dx) % W + W]

        sum_steps = []

        def add_term(chain, i):
            b, t0, n, ring, acc, res = chain
            if i < TERMS - 1:
                nc.vector.scalar_tensor_tensor(
                    out=acc[:, :, :, :], in0=shifted(ring, i), scalar=weight(i, b), in1=acc[:, :, :, :], op0=ALU.mult, op1=ALU.add
                )
                return
            for j in range(n):
                nc.vector.scalar_tensor_tensor(
                    out=res[:, j, :].rearrange("p (h w) -> p h w", w=W),
                    in0=shifted(ring, i)[:, :, j, :],
                    scalar=weight(i, b),
                    in1=acc[:, :, j, :],
                    op0=ALU.mult,
                    op1=ALU.add,
                )
            store(b, t0, n, res)

        def multiply_direct(b, t0, n):
            bank = psum.tile([P, BANK], F32, tag="bank")
            for j in range(n):
                channels = slice((t0 + j) * P, (t0 + j + 1) * P)
                mx_group(
                    bank[:, j * PIX : (j + 1) * PIX],
                    [(mw_part(g, channels), x_part(b, g, slice(0, PIX))) for g in range(PASSES)],
                )
            return (b, t0, n, bank)

        def fill_ring(b, t0, n, bank):
            ring = work.tile([P, H + 2 * REACH, PAIR, 2 * W], F32, name="ring", bufs=5)[:, :, 0:n, :]
            for j in range(n):
                m = bank[:, j * PIX : (j + 1) * PIX]
                for ring_row, image_row, rows in [(REACH, 0, H), (0, H - REACH, REACH), (REACH + H, 0, REACH)]:
                    nc.scalar.activation(
                        out=ring[:, ring_row : ring_row + rows, j, :].rearrange("p r (c w) -> p r c w", c=2),
                        in_=m[:, image_row * W : (image_row + rows) * W]
                        .rearrange("p (r w) -> p r w", w=W)
                        .unsqueeze(2)
                        .to_broadcast([P, rows, 2, W]),
                        func=ACT.Identity,
                        bias=mb_sb[:, t0 + j : t0 + j + 1],
                        scale=1.0,
                    )
            return (b, t0, n, ring)

        def first_term(b, t0, n, ring):
            acc = work.tile([P, H, PAIR, W], F32, name="acc", bufs=5)[:, :, 0:n, :]
            nc.scalar.activation(out=acc, in_=shifted(ring, 0), func=ACT.Copy, scale=weight(0, b))
            res = work.tile([P, PAIR, PIX], F32, name="res2", bufs=5)[:, 0:n, :]
            return (b, t0, n, ring, acc, res)

        def split(chain):
            b, t0, n, ring, acc, res = chain
            return [
                (b, t0 + j, 1, ring[:, :, j : j + 1, :], acc[:, :, j : j + 1, :], res[:, j : j + 1, :]) for j in range(n)
            ]

        def plan_sums(chains, first=1):
            for i in range(first, TERMS):
                for chain in chains:
                    sum_steps.append((chain, i))

        def add_terms(tiles):
            while tiles > 0 and sum_steps:
                chain, i = sum_steps[0]
                add_term(chain, i)
                sum_steps.remove(sum_steps[0])
                tiles -= chain[2]

        folded_tiles = dict()

        def multiply_group(b, t0, n_tiles):
            if t0 == 0:
                folded_tiles[b] = work.tile([P, 2, C], F32, name="folded", bufs=2)
            folded = folded_tiles[b]
            channels = slice(t0 * P, (t0 + n_tiles) * P)
            lower = [(x_part(b, g, slice(0, P)), mw_part(g, channels)) for g in range(PASSES)]
            upper = [(x_part(b, g, slice(P, 2 * P)), mw_part(g, channels)) for g in range(PASSES)]
            bank_sum = psum.tile([P, BANK], F32, tag="bank")
            mx_group(bank_sum[:, 0 : n_tiles * P], lower + upper)
            bank_lo = psum.tile([P, BANK], F32, tag="bank")
            mx_group(bank_lo[:, 0 : n_tiles * P], lower)
            return (folded, channels, bank_sum[:, 0 : n_tiles * P], bank_lo[:, 0 : n_tiles * P])

        def keep_sum(folded, channels, total, lo):
            nc.scalar.copy(out=folded[:, 0, channels], in_=total)

        def matrix_groups(b, size):
            return tile_groups(0, D_TILES - DIRECT_TILES[b], size)

        def subtract(folded, channels, total, lo):
            nc.vector.scalar_tensor_tensor(
                out=folded[:, 1, channels], in0=lo, scalar=2.0, in1=folded[:, 0, channels], op0=ALU.mult, op1=ALU.subtract
            )

        def apply_matrices(b, folded, t0, n_tiles):
            bank_u = psum.tile([P, BANK], F32, tag="bank")
            bank_v = psum.tile([P, BANK], F32, tag="bank")
            for sign, bank in enumerate((bank_u, bank_v)):
                for j in range(n_tiles):
                    t = t0 + j
                    nc.tensor.matmul(
                        out=bank[:, j * P : (j + 1) * P],
                        lhsT=folded[:, sign, t * P : (t + 1) * P],
                        rhs=matrix(b, sign),
                        start=True,
                        stop=True,
                    )
            u_sb = work.tile([P, GROUP, P], F32, name="u_sb", bufs=4)
            for j in range(n_tiles):
                t = t0 + j
                nc.scalar.activation(
                    out=u_sb[:, j, :],
                    in_=bank_u[:, j * P : (j + 1) * P],
                    func=ACT.Identity,
                    bias=mb_w[:, b, t : t + 1],
                    scale=1.0,
                )
            return (b, t0, n_tiles, u_sb, bank_v)

        def unfold(b, t0, n_tiles, u_sb, bank_v, behind_half):
            res = work.tile([P, n_tiles, PIX], F32, name="res_folded%d" % n_tiles, bufs=4 if n_tiles < GROUP else 3)
            for half, sign in enumerate((1.0, -1.0)):
                nc.vector.scalar_tensor_tensor(
                    out=res[:, :, half * P : (half + 1) * P],
                    in0=bank_v[:, 0 : n_tiles * P].rearrange("p (j c) -> p j c", j=n_tiles),
                    scalar=sign,
                    in1=u_sb[:, 0:n_tiles, :],
                    op0=ALU.mult,
                    op1=ALU.add,
                )
                behind_half()
            store(b, t0, n_tiles, res)


        load_mw(4, 2)
        park_strips()
        load_mw(6, 2)
        load_x(2)
        spread_matrices(matrix_images[:2])
        load_x(3)
        spread_matrices(matrix_images[2:])
        for b in range(4, B):
            load_x(b)
        regroup_x(0, nc.vector.tensor_copy, [1])
        mb_w = const.tile([P, B, D_TILES], F32)
        nc.vector.tensor_tensor(
            out=mb_w[:],
            in0=mb_sb[:].unsqueeze(1).to_broadcast([P, B, D_TILES]),
            in1=w_sum[:].unsqueeze(2).to_broadcast([P, B, D_TILES]),
            op=ALU.mult,
        )
        quantise_x(0)
        for t in range(4):
            transpose_mw(t, nc.scalar.copy)
        for t in (0, 1):
            quantise_mw(t, 1)
        ring = fill_ring(*multiply_direct(0, 0, 2))
        regroup_x(1, nc.vector.tensor_copy)
        quantise_mw(2, 2)
        quantise_x(1)
        transpose_mw(4, nc.scalar.copy)
        transpose_mw(5, nc.vector.tensor_copy)
        plan_sums([first_term(*ring)])
        product = multiply_direct(0, 2, 2)
        quantise_mw(4, 2)
        for t in (6, 7):
            transpose_mw(t, nc.scalar.copy)
        m1 = [multiply_group(1, 0, 4)]
        regroup_x(2, nc.scalar.copy, [1])
        keep_sum(*m1[0])
        ring = fill_ring(*product)
        regroup_x(2, nc.vector.tensor_copy, [0])
        quantise_mw(6, 2)
        add_terms(2)
        m1.append(multiply_group(1, 4, 4))
        keep_sum(*m1[1])
        plan_sums([first_term(*ring)])
        add_terms(2)
        subtract(*m1[0])
        add_terms(2)
        quantise_x(2)
        add_terms(2)
        subtract(*m1[1])
        add_terms(2)

        for b in range(1, B):
            nxt = matrix_groups(b + 1, GROUP) if b + 1 < B else []
            for g, (t0, n_tiles) in enumerate((matrix_groups(b, GROUP) if b + 1 < B else LAST_GROUPS)):
                part = apply_matrices(b, folded_tiles[b], t0, n_tiles)
                direct = None
                if g == 1 and b <= 3:
                    direct = multiply_direct(*((0, 2 + 2 * b, 2) if b < 3 else (3, 6, 2)))
                new = multiply_group(b + 1, *nxt[g]) if nxt else None
                ahead = g == 0 and b + 2 < B
                if ahead:
                    regroup_x(b + 2, nc.scalar.copy, [0])
                if direct:
                    ring = fill_ring(*direct)
                if new:
                    keep_sum(*new)
                if ahead:
                    regroup_x(b + 2, nc.scalar.copy, [1])
                if direct:
                    plan_sums([first_term(*ring)])
                unfold(*part, lambda: add_terms(2 if new else 2))
                if new:
                    subtract(*new)
                    add_terms(2)
                if g == 0 and b + 2 < B:
                    quantise_x(b + 2)
                    add_terms(2)
        add_terms(70)
